import numpy as np
import ml_dtypes


def mxq(x, axis, fmt="e4m3"):
    dtype, down = {"e4m3": (ml_dtypes.float8_e4m3fn, 7), "e5m2": (ml_dtypes.float8_e5m2, 14)}[fmt]
    v = np.moveaxis(np.asarray(x, np.float32).astype(ml_dtypes.bfloat16).astype(np.float64), axis, -1)
    blocks = v.reshape(v.shape[:-1] + (-1, 32))
    amax = np.abs(blocks).max(-1, keepdims=True)
    byte = np.maximum(np.where(amax > 0, np.frexp(amax)[1] - 1 + 127, 0) - down, 1)
    scale = np.exp2(byte - 127.0)
    codes = (blocks / scale).astype(np.float32).astype(dtype).astype(np.float64)
    return np.moveaxis((codes * scale).reshape(v.shape), -1, axis)


WIDE = False


def mx_kscale(k):
    if not WIDE:
        return np.ones(k)
    levels = np.array([10, -10, 5, -5, 0])
    if k % 512:
        return np.exp2(np.random.permutation(np.resize(levels, k // 32))).repeat(32)
    a = np.empty((k // 512, 16))
    for p in range(k // 512):
        a[p, :8] = np.random.permutation(np.resize(levels, 8))
        for g in range(8):
            far = levels[np.abs(levels - a[p, g]) >= 10]
            a[p, g + 8] = far[np.random.randint(len(far))]
    return np.exp2(a.ravel()).repeat(32)


BF16 = ml_dtypes.bfloat16


def bf(x):
    return np.asarray(x, np.float32).astype(BF16)


def f64(x):
    return np.asarray(x).astype(np.float64)


B, T, N, D, H, F = 2, 512, 4, 512, 8, 1024
S = B * N
EPS = 1e-5


def layernorm(v, g, b):
    mu = v.mean(-1, keepdims=True)
    var = np.square(v - mu).mean(-1, keepdims=True)
    return (v - mu) / np.sqrt(var + EPS) * g + b


def setup_inputs():
    s = mx_kscale(D)
    t = mx_kscale(D)
    return {"ax_cat": bf(np.random.standard_normal((S, T, D)) * 4.0 * s),
            "features": bf(np.random.standard_normal((B, T, N, D))),
            "wout_w": bf(np.random.standard_normal((D, D)) * 0.5 / np.sqrt(D) / s),
            "ln_g": bf((1.0 + 0.1 * np.random.standard_normal(D)) * t),
            "ln_b": bf(0.1 * np.random.standard_normal(D) * t),
            "ff1_w": bf(np.random.standard_normal((F, D)) / np.sqrt(D) / t),
            "ff1_b": bf(0.1 * np.random.standard_normal(F))}


def reference(ax_cat, features, wout_w, ln_g, ln_b, ff1_w, ff1_b):
    x = f64(features).transpose(0, 2, 1, 3).reshape(S, T, D)
    y = mxq(f64(ax_cat), 2, "e4m3") @ mxq(f64(wout_w), 1, "e4m3").T
    m = layernorm(y + x, f64(ln_g), f64(ln_b))
    return np.maximum((mxq(m, 2, "e4m3") @ mxq(f64(ff1_w), 1, "e4m3").T) + f64(ff1_b), 0.0)

@@ -1,0 +1,292 @@
+from contextlib import ExitStack
+
+import concourse.mybir as mybir
+from concourse.masks import make_identity
+
+F32 = mybir.dt.float32
+BF16 = mybir.dt.bfloat16
+U32 = mybir.dt.uint32
+U8 = mybir.dt.uint8
+FP8X4 = mybir.dt.float8_e4m3fn_x4
+ALU = mybir.AluOpType
+ACT = mybir.ActivationFunctionType
+
+P = 128
+PACK = 4
+BATCH, NODES = 2, 4
+SEQS = BATCH * NODES
+T = 512
+TILES = T // P
+D = 512
+F = 1024
+BANK = 512
+EPS = 1e-5
+PREPARE_ROUND = -3
+
+FLOPS = 2 * SEQS * T * D * (D + F)
+
+
+def tile_temporalatt_pb_t_kernel(tc, ax_cat, features, wout_w, ln_g, ln_b, ff1_w, ff1_b, out):
+    nc = tc.nc
+    with ExitStack() as stack:
+        const = stack.enter_context(tc.tile_pool(name="const", bufs=1))
+        inputs = stack.enter_context(tc.tile_pool(name="inputs", bufs=1))
+        work = stack.enter_context(tc.tile_pool(name="work", bufs=2))
+        stats = stack.enter_context(tc.tile_pool(name="stats", bufs=3))
+        results = stack.enter_context(tc.tile_pool(name="results", bufs=3))
+        ps_t = stack.enter_context(tc.psum_pool(name="ps_t", bufs=4))
+        ps_mx = stack.enter_context(tc.psum_pool(name="ps_mx", bufs=4))
+
+        ident_f32 = const.tile([P, P], F32)
+        make_identity(nc, ident_f32[:])
+        ident_bf16 = const.tile([P, P], BF16)
+        make_identity(nc, ident_bf16[:])
+        ones = const.tile([P, P], BF16)
+        nc.vector.memset(ones[:], 1.0)
+        eps = const.tile([P, 1], F32)
+        nc.vector.memset(eps[:], EPS)
+        warm = const.tile([P, 1], F32)
+        nc.scalar.activation(out=warm[:], in_=eps[:], func=ACT.Sqrt)
+
+        wout_sb = const.tile([P, D // P, D], BF16)
+        nc.sync.dma_start(out=wout_sb[:], in_=wout_w.rearrange("(p o) k -> p o k", o=PACK))
+        ax_sb = {}
+        x_sb = {}
+
+        def load_sequence(s):
+            ax_tile = inputs.tile([P, TILES, D], BF16, name="ax%d" % s)
+            nc.sync.dma_start(out=ax_tile[:], in_=ax_cat[s].rearrange("(p j) d -> p j d", j=TILES))
+            x_tile = inputs.tile([P, TILES, D], BF16, name="x%d" % s)
+            x_view = features[s // NODES].rearrange("(p j) n d -> p j n d", j=TILES)
+            nc.sync.dma_start(out=x_tile[:], in_=x_view[:, :, s % NODES, :])
+            ax_sb[s] = ax_tile
+            x_sb[s] = x_tile
+
+        load_sequence(0)
+        gain_rows = const.tile([P, PACK], BF16)
+        nc.sync.dma_start(out=gain_rows[:], in_=ln_g.rearrange("(p c) -> p c", c=PACK))
+        shift_rows = const.tile([P, PACK], BF16)
+        nc.sync.dma_start(out=shift_rows[:], in_=ln_b.rearrange("(p c) -> p c", c=PACK))
+        bias_row = const.tile([P, F], BF16)
+        nc.vector.memset(bias_row[:], 0.0)
+        nc.sync.dma_start(out=bias_row[0:1, :], in_=ff1_b.rearrange("(o f) -> o f", o=1))
+        ff1_sb = const.tile([P, F // P, D], BF16)
+        nc.sync.dma_start(out=ff1_sb[:], in_=ff1_w.rearrange("(o p) k -> p o k", p=P))
+        for s in range(1, SEQS):
+            load_sequence(s)
+
+        def transpose_rows(rows_sb):
+            grouped = work.tile([P, PACK * P, PACK], BF16, tag="grouped_rows", align_bytes=64)
+            grouped_words = grouped[:].bitcast(F32)
+            for half in range(2):
+                bank = ps_t.tile([P, 2, 2, P], F32, tag="t")
+                for i in range(2):
+                    words = rows_sb[:, 2 * half + i, :].bitcast(F32)
+                    for u in range(2):
+                        nc.tensor.transpose(bank[:, i, u, :], words[:, u::2], ident_f32[:])
+                nc.scalar.copy(
+                    out=grouped_words[:, half * 2 * P : (half + 1) * 2 * P, :].rearrange("p (i r) u -> p i r u", i=2),
+                    in_=bank[:].rearrange("p i u r -> p i r u"),
+                )
+            return grouped
+
+        def quantise(grouped, codes, scales):
+            nc.vector.quantize_mx(
+                out=codes[:].bitcast(FP8X4), scales=scales[:], in_=grouped[:].rearrange("p r t -> p (r t)")
+            )
+
+        wout_codes = const.tile([P, D], U32, align_bytes=64)
+        wout_scales = const.tile([P, D], U8, align_bytes=64)
+        wout_grouped = transpose_rows(wout_sb)
+        quantise(wout_grouped, wout_codes, wout_scales)
+
+        gain = const.tile([P, PACK], F32)
+        shift = const.tile([P, PACK], F32)
+        bias_all = const.tile([P, F], F32)
+        ff1_grouped = const.tile([P, F, PACK], BF16, align_bytes=64)
+        ff1_codes = const.tile([P, F], U32, align_bytes=64)
+        ff1_scales = const.tile([P, F], U8, align_bytes=64)
+
+        def prepare_second_layer():
+            nc.vector.tensor_copy(out=gain[:], in_=gain_rows[:])
+            nc.vector.tensor_copy(out=shift[:], in_=shift_rows[:])
+            for pair in range(F // (2 * P)):
+                bank = ps_t.tile([P, 2, PACK, P], BF16, tag="t")
+                for i in range(2):
+                    for c in range(PACK):
+                        nc.tensor.transpose(
+                            bank[:, i, c, :], ff1_sb[:, 2 * pair + i, c::PACK], ident_bf16[:]
+                        )
+                nc.scalar.copy(
+                    out=ff1_grouped[:, pair * 2 * P : (pair + 1) * 2 * P, :].rearrange("p (i f) c -> p i f c", i=2),
+                    in_=bank[:].rearrange("p i c f -> p i f c"),
+                )
+            quantise(ff1_grouped, ff1_codes, ff1_scales)
+            for h in range(F // BANK):
+                bias_bank = ps_mx.tile([P, BANK], F32, tag="mx")
+                nc.tensor.matmul(
+                    out=bias_bank[:], lhsT=ones[:], rhs=bias_row[:, h * BANK : (h + 1) * BANK], start=True, stop=True
+                )
+                nc.scalar.copy(out=bias_all[:, h * BANK : (h + 1) * BANK], in_=bias_bank[:])
+
+        ax_grouped = {}
+        ax_codes = {}
+        ax_scales = {}
+        residual = {}
+        row_sum = {}
+        neg_mean = {}
+        std = {}
+        rstd = {}
+        m_planes = {}
+        m_codes = {}
+        m_scales = {}
+
+        def ax_transpose(s):
+            ax_grouped[s] = transpose_rows(ax_sb[s])
+
+        def ax_quantise(s):
+            codes = work.tile([P, T], U32, tag="ax_codes", align_bytes=64)
+            scales = work.tile([P, T], U8, tag="ax_scales", align_bytes=64)
+            quantise(ax_grouped[s], codes, scales)
+            ax_codes[s] = codes
+            ax_scales[s] = scales
+
+        def project(s):
+            r = work.tile([P, TILES, D], F32, tag="r", bufs=4)
+            sums = stats.tile([P, TILES], F32, tag="sums")
+            for j in range(TILES):
+                y = ps_mx.tile([P, D], F32, tag="mx")
+                nc.tensor.matmul_mx(
+                    out=y[:],
+                    lhsT=ax_codes[s][:, j * P : (j + 1) * P].bitcast(FP8X4),
+                    lhsT_scale=ax_scales[s][:, j * P : (j + 1) * P],
+                    rhs=wout_codes[:].bitcast(FP8X4),
+                    rhs_scale=wout_scales[:],
+                    start=True,
+                    stop=True,
+                )
+                nc.vector.scalar_tensor_tensor(
+                    out=r[:, j, :].rearrange("p (t i) -> p t i", t=PACK),
+                    in0=y[:].rearrange("p (t i) -> p t i", t=PACK),
+                    scalar=1.0,
+                    in1=x_sb[s][:, j, :].rearrange("p (i t) -> p t i", t=PACK),
+                    op0=ALU.mult,
+                    op1=ALU.add,
+                    accum_out=sums[:, j : j + 1],
+                )
+            residual[s] = r
+            row_sum[s] = sums
+
+        def statistics(s):
+            minus = stats.tile([P, TILES], F32, tag="neg_mean")
+            nc.scalar.mul(out=minus[:], in_=row_sum[s][:], mul=-1.0 / D)
+            squares = work.tile([P, TILES, D], BF16, tag="squares", bufs=1)
+            sum_sq = stats.tile([P, TILES], F32, tag="sum_sq")
+            for j in range(TILES):
+                nc.scalar.activation(
+                    out=squares[:, j, :],
+                    in_=residual[s][:, j, :],
+                    func=ACT.Square,
+                    bias=minus[:, j : j + 1],
+                    scale=1.0,
+                    accum_out=sum_sq[:, j : j + 1],
+                )
+            root = stats.tile([P, TILES], F32, tag="std")
+            nc.scalar.activation(out=root[:], in_=sum_sq[:], func=ACT.Sqrt, bias=eps[:], scale=1.0 / D)
+            neg_mean[s] = minus
+            std[s] = root
+
+        def inverse_std(s):
+            inverse = stats.tile([P, TILES], F32, tag="rstd")
+            nc.vector.reciprocal(out=inverse[:], in_=std[s][:])
+            rstd[s] = inverse
+
+        def normalise(s):
+            for j in range(TILES):
+                nc.gpsimd.tensor_scalar(
+                    out=residual[s][:, j, :],
+                    in0=residual[s][:, j, :],
+                    scalar1=neg_mean[s][:, j : j + 1],
+                    scalar2=rstd[s][:, j : j + 1],
+                    op0=ALU.add,
+                    op1=ALU.mult,
+                )
+
+        def m_transpose(s):
+            planes = work.tile([P, PACK, T], BF16, tag="planes")
+            for c in range(PACK):
+                bank = ps_t.tile([P, TILES, P], F32, tag="t")
+                for j in range(TILES):
+                    nc.tensor.transpose(bank[:, j, :], residual[s][:, j, c * P : (c + 1) * P], ident_f32[:])
+                nc.scalar.activation(
+                    out=planes[:, c, :],
+                    in_=bank[:].rearrange("p j t -> p (j t)"),
+                    func=ACT.Identity,
+                    bias=shift[:, c : c + 1],
+                    scale=gain[:, c : c + 1],
+                )
+            m_planes[s] = planes
+
+        def m_quantise(s):
+            grouped = work.tile([P, T, PACK], BF16, tag="grouped_m", align_bytes=64)
+            nc.vector.tensor_copy(
+                out=grouped[:].rearrange("p (w i) c -> p w c i", i=4),
+                in_=m_planes[s][:].rearrange("p c (w i) -> p w c i", i=4),
+            )
+            codes = work.tile([P, T], U32, tag="m_codes", align_bytes=64)
+            scales = work.tile([P, T], U8, tag="m_scales", align_bytes=64)
+            quantise(grouped, codes, scales)
+            m_codes[s] = codes
+            m_scales[s] = scales
+
+        def feed_forward(s):
+            result = results.tile([P, TILES, F], F32, tag="result")
+            out_view = out[s].rearrange("(p j) f -> p j f", j=TILES)
+            for j in range(TILES):
+                for h in range(F // BANK):
+                    acc = ps_mx.tile([P, BANK], F32, tag="mx")
+                    nc.tensor.matmul_mx(
+                        out=acc[:],
+                        lhsT=m_codes[s][:, j * P : (j + 1) * P].bitcast(FP8X4),
+                        lhsT_scale=m_scales[s][:, j * P : (j + 1) * P],
+                        rhs=ff1_codes[:, h * BANK : (h + 1) * BANK].bitcast(FP8X4),
+                        rhs_scale=ff1_scales[:, h * BANK : (h + 1) * BANK],
+                        start=True,
+                        stop=True,
+                    )
+                    nc.vector.tensor_tensor(
+                        out=result[:, j, h * BANK : (h + 1) * BANK],
+                        in0=acc[:],
+                        in1=bias_all[:, h * BANK : (h + 1) * BANK],
+                        op=ALU.add,
+                    )
+                if j < TILES - 1:
+                    nc.scalar.activation(out=result[:, j, :], in_=result[:, j, :], func=ACT.Relu)
+                else:
+                    nc.vector.tensor_scalar_max(out=result[:, j, :], in0=result[:, j, :], scalar1=0.0)
+                nc.sync.dma_start(out=out_view[:, j, :], in_=result[:, j, :])
+
+        def live(s):
+            return 0 <= s < SEQS
+
+        for i in range(-6, SEQS):
+            if live(i + 2):
+                inverse_std(i + 2)
+            if live(i + 4):
+                project(i + 4)
+            if live(i + 1):
+                m_transpose(i + 1)
+            if live(i + 6):
+                ax_transpose(i + 6)
+            if live(i + 2):
+                normalise(i + 2)
+            if live(i + 5):
+                ax_quantise(i + 5)
+            if live(i):
+                m_quantise(i)
+            if live(i + 3):
+                statistics(i + 3)
+            if i == PREPARE_ROUND:
+                prepare_second_layer()
+            if live(i):
+                feed_forward(i)

@@ -203,7 +203,7 @@ def tile_temporalatt_pb_t_kernel(tc, ax_cat, features, wout_w, ln_g, ln_b, ff1_w
 
         def normalise(s):
             for j in range(TILES):
-                nc.gpsimd.tensor_scalar(
+                nc.vector.tensor_scalar(
                     out=residual[s][:, j, :],
                     in0=residual[s][:, j, :],
                     scalar1=neg_mean[s][:, j : j + 1],
@@ -260,10 +260,7 @@ def tile_temporalatt_pb_t_kernel(tc, ax_cat, features, wout_w, ln_g, ln_b, ff1_w
                         in1=bias_all[:, h * BANK : (h + 1) * BANK],
                         op=ALU.add,
                     )
-                if j < TILES - 1:
-                    nc.scalar.activation(out=result[:, j, :], in_=result[:, j, :], func=ACT.Relu)
-                else:
-                    nc.vector.tensor_scalar_max(out=result[:, j, :], in0=result[:, j, :], scalar1=0.0)
+                nc.scalar.activation(out=result[:, j, :], in_=result[:, j, :], func=ACT.Relu)
                 nc.sync.dma_start(out=out_view[:, j, :], in_=result[:, j, :])
 
         def live(s):

@@ -16,12 +16,15 @@ PACK = 4
 BATCH, NODES = 2, 4
 SEQS = BATCH * NODES
 T = 512
-TILES = T // P
 D = 512
 F = 1024
 BANK = 512
 EPS = 1e-5
-PREPARE_ROUND = -3
+F32_MAX = 3.4028234663852886e38
+TILES = 2
+TOKENS = TILES * P
+PARTS = T // TOKENS
+UNITS = SEQS * PARTS
 
 FLOPS = 2 * SEQS * T * D * (D + F)
 
@@ -31,259 +34,295 @@ def tile_temporalatt_pb_t_kernel(tc, ax_cat, features, wout_w, ln_g, ln_b, ff1_w
     with ExitStack() as stack:
         const = stack.enter_context(tc.tile_pool(name="const", bufs=1))
         inputs = stack.enter_context(tc.tile_pool(name="inputs", bufs=1))
-        work = stack.enter_context(tc.tile_pool(name="work", bufs=2))
-        stats = stack.enter_context(tc.tile_pool(name="stats", bufs=3))
-        results = stack.enter_context(tc.tile_pool(name="results", bufs=3))
+        work = stack.enter_context(tc.tile_pool(name="work", bufs=3))
+        stats = stack.enter_context(tc.tile_pool(name="stats", bufs=6))
+        results = stack.enter_context(tc.tile_pool(name="results", bufs=4))
         ps_t = stack.enter_context(tc.psum_pool(name="ps_t", bufs=4))
         ps_mx = stack.enter_context(tc.psum_pool(name="ps_mx", bufs=4))
+        stack.enter_context(tc.manual_schedule())
 
         ident_f32 = const.tile([P, P], F32)
         make_identity(nc, ident_f32[:])
-        ident_bf16 = const.tile([P, P], BF16)
-        make_identity(nc, ident_bf16[:])
         ones = const.tile([P, P], BF16)
         nc.vector.memset(ones[:], 1.0)
         eps = const.tile([P, 1], F32)
         nc.vector.memset(eps[:], EPS)
         warm = const.tile([P, 1], F32)
         nc.scalar.activation(out=warm[:], in_=eps[:], func=ACT.Sqrt)
+        bias_row = const.tile([P, F], BF16)
+        nc.vector.memset(bias_row[:], 0.0)
 
-        wout_sb = const.tile([P, D // P, D], BF16)
-        nc.sync.dma_start(out=wout_sb[:], in_=wout_w.rearrange("(p o) k -> p o k", o=PACK))
+        wout_sb = const.tile([P, PACK, D], BF16)
+        wout_view = wout_w.rearrange("(p o) k -> p o k", o=PACK)
         ax_sb = {}
         x_sb = {}
 
-        def load_sequence(s):
-            ax_tile = inputs.tile([P, TILES, D], BF16, name="ax%d" % s)
-            nc.sync.dma_start(out=ax_tile[:], in_=ax_cat[s].rearrange("(p j) d -> p j d", j=TILES))
-            x_tile = inputs.tile([P, TILES, D], BF16, name="x%d" % s)
-            x_view = features[s // NODES].rearrange("(p j) n d -> p j n d", j=TILES)
-            nc.sync.dma_start(out=x_tile[:], in_=x_view[:, :, s % NODES, :])
-            ax_sb[s] = ax_tile
-            x_sb[s] = x_tile
+        def load_ax(u):
+            ax_tile = inputs.tile([P, TILES, D], BF16, name="ax%d" % u)
+            ax_view = ax_cat[u // PARTS].rearrange("(h p j) d -> h p j d", h=PARTS, j=TILES)
+            nc.sync.dma_start(out=ax_tile[:], in_=ax_view[u % PARTS])
+            ax_sb[u] = ax_tile
 
-        load_sequence(0)
+        def load_x(u):
+            s = u // PARTS
+            x_tile = inputs.tile([P, TILES, D], BF16, name="x%d" % u)
+            x_view = features[s // NODES].rearrange("(h p j) n d -> h p j n d", h=PARTS, j=TILES)
+            nc.sync.dma_start(out=x_tile[:], in_=x_view[u % PARTS][:, :, s % NODES, :])
+            x_sb[u] = x_tile
+
+        nc.sync.dma_start(out=wout_sb[:], in_=wout_view)
+        load_ax(0)
+        load_x(0)
+        load_ax(1)
         gain_rows = const.tile([P, PACK], BF16)
         nc.sync.dma_start(out=gain_rows[:], in_=ln_g.rearrange("(p c) -> p c", c=PACK))
         shift_rows = const.tile([P, PACK], BF16)
         nc.sync.dma_start(out=shift_rows[:], in_=ln_b.rearrange("(p c) -> p c", c=PACK))
-        bias_row = const.tile([P, F], BF16)
-        nc.vector.memset(bias_row[:], 0.0)
         nc.sync.dma_start(out=bias_row[0:1, :], in_=ff1_b.rearrange("(o f) -> o f", o=1))
+        load_x(1)
         ff1_sb = const.tile([P, F // P, D], BF16)
-        nc.sync.dma_start(out=ff1_sb[:], in_=ff1_w.rearrange("(o p) k -> p o k", p=P))
-        for s in range(1, SEQS):
-            load_sequence(s)
+        for q in range(2):
+            nc.sync.dma_start(
+                out=ff1_sb[:, 4 * q : 4 * q + 4, :], in_=ff1_w[512 * q : 512 * (q + 1), :].rearrange("(o p) k -> p o k", p=P)
+            )
+        for u in range(2, UNITS):
+            load_ax(u)
+            load_x(u)
 
-        def transpose_rows(rows_sb):
-            grouped = work.tile([P, PACK * P, PACK], BF16, tag="grouped_rows", align_bytes=64)
-            grouped_words = grouped[:].bitcast(F32)
-            for half in range(2):
-                bank = ps_t.tile([P, 2, 2, P], F32, tag="t")
-                for i in range(2):
-                    words = rows_sb[:, 2 * half + i, :].bitcast(F32)
-                    for u in range(2):
-                        nc.tensor.transpose(bank[:, i, u, :], words[:, u::2], ident_f32[:])
-                nc.scalar.copy(
-                    out=grouped_words[:, half * 2 * P : (half + 1) * 2 * P, :].rearrange("p (i r) u -> p i r u", i=2),
-                    in_=bank[:].rearrange("p i u r -> p i r u"),
-                )
-            return grouped
+        def transpose_pair(rows_sb, i, grouped, engine):
+            bank = ps_t.tile([P, 2, 2, P], F32, tag="t")
+            for r in range(2):
+                words = rows_sb[:, i + r, :].bitcast(F32)
+                for w in range(2):
+                    nc.tensor.transpose(bank[:, r, w, :], words[:, w::2], ident_f32[:])
+            engine(
+                out=grouped[:, i * P : (i + 2) * P, :]
+                .rearrange("p n c -> p (n c)")
+                .bitcast(F32)
+                .rearrange("p (i r w) -> p i r w", i=2, w=2),
+                in_=bank[:].rearrange("p i w r -> p i r w"),
+            )
 
         def quantise(grouped, codes, scales):
             nc.vector.quantize_mx(
-                out=codes[:].bitcast(FP8X4), scales=scales[:], in_=grouped[:].rearrange("p r t -> p (r t)")
+                out=codes.bitcast(FP8X4), scales=scales, in_=grouped.rearrange("p r t -> p (r t)")
             )
 
+        wout_grouped = const.tile([P, D, PACK], BF16, align_bytes=64)
         wout_codes = const.tile([P, D], U32, align_bytes=64)
         wout_scales = const.tile([P, D], U8, align_bytes=64)
-        wout_grouped = transpose_rows(wout_sb)
-        quantise(wout_grouped, wout_codes, wout_scales)
-
         gain = const.tile([P, PACK], F32)
         shift = const.tile([P, PACK], F32)
         bias_all = const.tile([P, F], F32)
-        ff1_grouped = const.tile([P, F, PACK], BF16, align_bytes=64)
-        ff1_codes = const.tile([P, F], U32, align_bytes=64)
-        ff1_scales = const.tile([P, F], U8, align_bytes=64)
+        ff1_grouped = [const.tile([P, BANK, PACK], BF16, name="ff1_grouped%d" % h, align_bytes=64) for h in range(2)]
+        ff1_codes = [const.tile([P, BANK], U32, name="ff1_codes%d" % h, align_bytes=64) for h in range(2)]
+        ff1_scales = [const.tile([P, BANK], U8, name="ff1_scales%d" % h, align_bytes=64) for h in range(2)]
 
-        def prepare_second_layer():
-            nc.vector.tensor_copy(out=gain[:], in_=gain_rows[:])
-            nc.vector.tensor_copy(out=shift[:], in_=shift_rows[:])
-            for pair in range(F // (2 * P)):
-                bank = ps_t.tile([P, 2, PACK, P], BF16, tag="t")
-                for i in range(2):
-                    for c in range(PACK):
-                        nc.tensor.transpose(
-                            bank[:, i, c, :], ff1_sb[:, 2 * pair + i, c::PACK], ident_bf16[:]
-                        )
-                nc.scalar.copy(
-                    out=ff1_grouped[:, pair * 2 * P : (pair + 1) * 2 * P, :].rearrange("p (i f) c -> p i f c", i=2),
-                    in_=bank[:].rearrange("p i c f -> p i f c"),
-                )
-            quantise(ff1_grouped, ff1_codes, ff1_scales)
-            for h in range(F // BANK):
-                bias_bank = ps_mx.tile([P, BANK], F32, tag="mx")
-                nc.tensor.matmul(
-                    out=bias_bank[:], lhsT=ones[:], rhs=bias_row[:, h * BANK : (h + 1) * BANK], start=True, stop=True
-                )
-                nc.scalar.copy(out=bias_all[:, h * BANK : (h + 1) * BANK], in_=bias_bank[:])
+        transpose_pair(wout_sb, 0, wout_grouped, nc.scalar.copy)
+        transpose_pair(wout_sb, 2, wout_grouped, nc.vector.tensor_copy)
+        quantise(wout_grouped[:], wout_codes[:], wout_scales[:])
 
         ax_grouped = {}
         ax_codes = {}
         ax_scales = {}
         residual = {}
         row_sum = {}
+        sum_sq = {}
         neg_mean = {}
         std = {}
         rstd = {}
         m_planes = {}
+        m_grouped = {}
         m_codes = {}
         m_scales = {}
+        result = {}
 
-        def ax_transpose(s):
-            ax_grouped[s] = transpose_rows(ax_sb[s])
+        def ax_transpose(u, k):
+            if k == 0:
+                fresh_ax_grouped = work.tile([P, TOKENS, PACK], BF16, tag="ax_grouped", align_bytes=64)
+                ax_grouped[u] = fresh_ax_grouped
+            transpose_pair(ax_sb[u], 2 * k, ax_grouped[u], nc.scalar.copy);
 
-        def ax_quantise(s):
-            codes = work.tile([P, T], U32, tag="ax_codes", align_bytes=64)
-            scales = work.tile([P, T], U8, tag="ax_scales", align_bytes=64)
-            quantise(ax_grouped[s], codes, scales)
-            ax_codes[s] = codes
-            ax_scales[s] = scales
+        def ax_quantise(u):
+            fresh_ax_codes = work.tile([P, TOKENS], U32, tag="ax_codes", align_bytes=64)
+            ax_codes[u] = fresh_ax_codes
+            fresh_ax_scales = work.tile([P, TOKENS], U8, tag="ax_scales", align_bytes=64)
+            ax_scales[u] = fresh_ax_scales
+            quantise(ax_grouped[u][:], ax_codes[u][:], ax_scales[u][:])
 
-        def project(s):
-            r = work.tile([P, TILES, D], F32, tag="r", bufs=4)
-            sums = stats.tile([P, TILES], F32, tag="sums")
-            for j in range(TILES):
-                y = ps_mx.tile([P, D], F32, tag="mx")
-                nc.tensor.matmul_mx(
-                    out=y[:],
-                    lhsT=ax_codes[s][:, j * P : (j + 1) * P].bitcast(FP8X4),
-                    lhsT_scale=ax_scales[s][:, j * P : (j + 1) * P],
-                    rhs=wout_codes[:].bitcast(FP8X4),
-                    rhs_scale=wout_scales[:],
-                    start=True,
-                    stop=True,
-                )
-                nc.vector.scalar_tensor_tensor(
-                    out=r[:, j, :].rearrange("p (t i) -> p t i", t=PACK),
-                    in0=y[:].rearrange("p (t i) -> p t i", t=PACK),
-                    scalar=1.0,
-                    in1=x_sb[s][:, j, :].rearrange("p (i t) -> p t i", t=PACK),
-                    op0=ALU.mult,
-                    op1=ALU.add,
-                    accum_out=sums[:, j : j + 1],
-                )
-            residual[s] = r
-            row_sum[s] = sums
+        def project(u, j):
+            if j == 0:
+                fresh_residual = work.tile([P, TILES, D], F32, tag="r", bufs=6)
+                residual[u] = fresh_residual
+                fresh_row_sum = stats.tile([P, TILES], F32, tag="sums")
+                row_sum[u] = fresh_row_sum
+                fresh_sum_sq = stats.tile([P, TILES], F32, tag="sum_sq")
+                sum_sq[u] = fresh_sum_sq
+            y = ps_mx.tile([P, D], F32, tag="mx")
+            nc.tensor.matmul_mx(
+                out=y[:],
+                lhsT=ax_codes[u][:, j * P : (j + 1) * P].bitcast(FP8X4),
+                lhsT_scale=ax_scales[u][:, j * P : (j + 1) * P],
+                rhs=wout_codes[:].bitcast(FP8X4),
+                rhs_scale=wout_scales[:],
+                start=True,
+                stop=True,
+            )
+            nc.vector.scalar_tensor_tensor(
+                out=residual[u][:, j, :].rearrange("p (t i) -> p t i", t=PACK),
+                in0=y[:].rearrange("p (t i) -> p t i", t=PACK),
+                scalar=1.0,
+                in1=x_sb[u][:, j, :].rearrange("p (i t) -> p t i", t=PACK),
+                op0=ALU.mult,
+                op1=ALU.add,
+                accum_out=row_sum[u][:, j : j + 1],
+            )
 
-        def statistics(s):
-            minus = stats.tile([P, TILES], F32, tag="neg_mean")
-            nc.scalar.mul(out=minus[:], in_=row_sum[s][:], mul=-1.0 / D)
-            squares = work.tile([P, TILES, D], BF16, tag="squares", bufs=1)
-            sum_sq = stats.tile([P, TILES], F32, tag="sum_sq")
-            for j in range(TILES):
-                nc.scalar.activation(
-                    out=squares[:, j, :],
-                    in_=residual[s][:, j, :],
-                    func=ACT.Square,
-                    bias=minus[:, j : j + 1],
-                    scale=1.0,
-                    accum_out=sum_sq[:, j : j + 1],
-                )
+        def square(u, j):
+            squares = work.tile([P, D], BF16, tag="squares", bufs=2)
+            nc.scalar.activation(
+                out=squares[:],
+                in_=residual[u][:, j, :],
+                func=ACT.Square,
+                bias=row_sum[u][:, j : j + 1],
+                scale=-float(D),
+                accum_out=sum_sq[u][:, j : j + 1],
+            )
+
+        def finish_statistics(u):
+            fresh_neg_mean = stats.tile([P, TILES], F32, tag="neg_mean")
+            neg_mean[u] = fresh_neg_mean
+            nc.gpsimd.tensor_scalar(
+                out=neg_mean[u][:], in0=row_sum[u][:], scalar1=-1.0 / D, scalar2=0.0, op0=ALU.mult, op1=ALU.add
+            )
             root = stats.tile([P, TILES], F32, tag="std")
-            nc.scalar.activation(out=root[:], in_=sum_sq[:], func=ACT.Sqrt, bias=eps[:], scale=1.0 / D)
-            neg_mean[s] = minus
-            std[s] = root
+            nc.scalar.activation(out=root[:], in_=sum_sq[u][:], func=ACT.Sqrt, bias=eps[:], scale=1.0 / D**3)
+            std[u] = root
 
-        def inverse_std(s):
-            inverse = stats.tile([P, TILES], F32, tag="rstd")
-            nc.vector.reciprocal(out=inverse[:], in_=std[s][:])
-            rstd[s] = inverse
+        def invert(u):
+            fresh_rstd = stats.tile([P, TILES], F32, tag="rstd")
+            rstd[u] = fresh_rstd
+            nc.vector.reciprocal(out=rstd[u][:], in_=std[u][:])
 
-        def normalise(s):
-            for j in range(TILES):
-                nc.vector.tensor_scalar(
-                    out=residual[s][:, j, :],
-                    in0=residual[s][:, j, :],
-                    scalar1=neg_mean[s][:, j : j + 1],
-                    scalar2=rstd[s][:, j : j + 1],
-                    op0=ALU.add,
-                    op1=ALU.mult,
-                )
+        def normalise(u, j):
+            nc.vector.tensor_scalar(
+                out=residual[u][:, j, :],
+                in0=residual[u][:, j, :],
+                scalar1=neg_mean[u][:, j : j + 1],
+                scalar2=rstd[u][:, j : j + 1],
+                op0=ALU.add,
+                op1=ALU.mult,
+            )
 
-        def m_transpose(s):
-            planes = work.tile([P, PACK, T], BF16, tag="planes")
-            for c in range(PACK):
-                bank = ps_t.tile([P, TILES, P], F32, tag="t")
+        def m_transpose(u, k):
+            if k == 0:
+                fresh_m_planes = work.tile([P, PACK, TOKENS], BF16, tag="planes")
+                m_planes[u] = fresh_m_planes
+            group = BANK // TOKENS
+            bank = ps_t.tile([P, group, TILES, P], F32, tag="t")
+            for i in range(group):
+                c = k * group + i
                 for j in range(TILES):
-                    nc.tensor.transpose(bank[:, j, :], residual[s][:, j, c * P : (c + 1) * P], ident_f32[:])
+                    nc.tensor.transpose(bank[:, i, j, :], residual[u][:, j, c * P : (c + 1) * P], ident_f32[:])
+            for i in range(group):
+                c = k * group + i
                 nc.scalar.activation(
-                    out=planes[:, c, :],
-                    in_=bank[:].rearrange("p j t -> p (j t)"),
+                    out=m_planes[u][:, c, :],
+                    in_=bank[:, i, :, :].rearrange("p j t -> p (j t)"),
                     func=ACT.Identity,
                     bias=shift[:, c : c + 1],
                     scale=gain[:, c : c + 1],
                 )
-            m_planes[s] = planes
 
-        def m_quantise(s):
-            grouped = work.tile([P, T, PACK], BF16, tag="grouped_m", align_bytes=64)
+        def m_interleave(u):
+            fresh_m_grouped = work.tile([P, TOKENS, PACK], BF16, tag="grouped_m", align_bytes=64)
+            m_grouped[u] = fresh_m_grouped
             nc.vector.tensor_copy(
-                out=grouped[:].rearrange("p (w i) c -> p w c i", i=4),
-                in_=m_planes[s][:].rearrange("p c (w i) -> p w c i", i=4),
+                out=m_grouped[u][:].rearrange("p (w i) c -> p w c i", i=4),
+                in_=m_planes[u][:].rearrange("p c (w i) -> p w c i", i=4),
             )
-            codes = work.tile([P, T], U32, tag="m_codes", align_bytes=64)
-            scales = work.tile([P, T], U8, tag="m_scales", align_bytes=64)
-            quantise(grouped, codes, scales)
-            m_codes[s] = codes
-            m_scales[s] = scales
 
-        def feed_forward(s):
-            result = results.tile([P, TILES, F], F32, tag="result")
-            out_view = out[s].rearrange("(p j) f -> p j f", j=TILES)
-            for j in range(TILES):
-                for h in range(F // BANK):
-                    acc = ps_mx.tile([P, BANK], F32, tag="mx")
-                    nc.tensor.matmul_mx(
-                        out=acc[:],
-                        lhsT=m_codes[s][:, j * P : (j + 1) * P].bitcast(FP8X4),
-                        lhsT_scale=m_scales[s][:, j * P : (j + 1) * P],
-                        rhs=ff1_codes[:, h * BANK : (h + 1) * BANK].bitcast(FP8X4),
-                        rhs_scale=ff1_scales[:, h * BANK : (h + 1) * BANK],
-                        start=True,
-                        stop=True,
-                    )
-                    nc.vector.tensor_tensor(
-                        out=result[:, j, h * BANK : (h + 1) * BANK],
-                        in0=acc[:],
-                        in1=bias_all[:, h * BANK : (h + 1) * BANK],
-                        op=ALU.add,
-                    )
-                nc.scalar.activation(out=result[:, j, :], in_=result[:, j, :], func=ACT.Relu)
-                nc.sync.dma_start(out=out_view[:, j, :], in_=result[:, j, :])
+        def m_quantise(u):
+            fresh_m_codes = work.tile([P, TOKENS], U32, tag="m_codes", align_bytes=64)
+            m_codes[u] = fresh_m_codes
+            fresh_m_scales = work.tile([P, TOKENS], U8, tag="m_scales", align_bytes=64)
+            m_scales[u] = fresh_m_scales
+            quantise(m_grouped[u][:], m_codes[u][:], m_scales[u][:])
 
-        def live(s):
-            return 0 <= s < SEQS
+        def feed_forward(u, k):
+            j, h = divmod(k, 2)
+            if k == 0:
+                fresh_result = results.tile([P, TILES, F], F32, tag="result")
+                result[u] = fresh_result
+            acc = ps_mx.tile([P, BANK], F32, tag="mx")
+            nc.tensor.matmul_mx(
+                out=acc[:],
+                lhsT=m_codes[u][:, j * P : (j + 1) * P].bitcast(FP8X4),
+                lhsT_scale=m_scales[u][:, j * P : (j + 1) * P],
+                rhs=ff1_codes[h][:].bitcast(FP8X4),
+                rhs_scale=ff1_scales[h][:],
+                start=True,
+                stop=True,
+            )
+            nc.vector.tensor_tensor(
+                out=result[u][:, j, h * BANK : (h + 1) * BANK],
+                in0=acc[:],
+                in1=bias_all[:, h * BANK : (h + 1) * BANK],
+                op=ALU.add,
+            )
 
-        for i in range(-6, SEQS):
-            if live(i + 2):
-                inverse_std(i + 2)
-            if live(i + 4):
-                project(i + 4)
-            if live(i + 1):
-                m_transpose(i + 1)
-            if live(i + 6):
-                ax_transpose(i + 6)
-            if live(i + 2):
-                normalise(i + 2)
-            if live(i + 5):
-                ax_quantise(i + 5)
-            if live(i):
-                m_quantise(i)
-            if live(i + 3):
-                statistics(i + 3)
-            if i == PREPARE_ROUND:
-                prepare_second_layer()
-            if live(i):
-                feed_forward(i)
+        def relu_store(u, j):
+            tile = result[u][:, j, :]
+            which = ["S","S","S","S"][(u * TILES + j) % 4]
+            if which == "S":
+                nc.scalar.activation(out=tile, in_=tile, func=ACT.Relu)
+            elif which == "V":
+                nc.vector.tensor_scalar_max(out=tile, in0=tile, scalar1=0.0)
+            else:
+                nc.gpsimd.tensor_scalar(out=tile, in0=tile, scalar1=F32_MAX, scalar2=0.0, op0=ALU.min, op1=ALU.max)
+            out_view = out[u // PARTS].rearrange("(h p j) f -> h p j f", h=PARTS, j=TILES)[u % PARTS]
+            nc.sync.dma_start(out=out_view[:, j, :], in_=tile)
+
+        def prepare_vectors():
+            nc.vector.tensor_copy(out=gain[:], in_=gain_rows[:])
+            nc.vector.tensor_copy(out=shift[:], in_=shift_rows[:])
+
+        def prepare_bias(h):
+            bias_bank = ps_mx.tile([P, BANK], F32, tag="mx")
+            nc.tensor.matmul(
+                out=bias_bank[:], lhsT=ones[:], rhs=bias_row[:, h * BANK : (h + 1) * BANK], start=True, stop=True
+            )
+            nc.scalar.copy(out=bias_all[:, h * BANK : (h + 1) * BANK], in_=bias_bank[:])
+
+        def prepare_ff1(k):
+            h, i = divmod(k, 2)
+            transpose_pair(ff1_sb[:, 4 * h : 4 * h + 4, :], 2 * i, ff1_grouped[h], nc.scalar.copy if i == 0 else nc.vector.tensor_copy)
+
+        def quantise_ff1(h):
+            quantise(ff1_grouped[h][:], ff1_codes[h][:], ff1_scales[h][:])
+
+        atoms = []
+
+        def add(at, spread, n, make):
+            for k in range(n):
+                atoms.append((at + spread * (k + 0.5) / n, len(atoms), make(k)))
+
+        for u in range(UNITS):
+            add(u + 0, 0.5, TILES // 2, lambda k, u=u: lambda: ax_transpose(u, k))
+            add(u + 0.75, 0, 1, lambda k, u=u: lambda: ax_quantise(u))
+            add(u + 1, 1, TILES, lambda k, u=u: lambda: project(u, k))
+            add(u + 1.3, 1, TILES, lambda k, u=u: lambda: square(u, k))
+            add(u + 2.35, 0, 1, lambda k, u=u: lambda: finish_statistics(u))
+            add(u + 2.7, 0, 1, lambda k, u=u: lambda: invert(u))
+            add(u + 2.75, 0.5, TILES, lambda k, u=u: lambda: normalise(u, k))
+            add(u + 3.3, 0.7, TILES, lambda k, u=u: lambda: m_transpose(u, k))
+            add(u + 4.2, 0, 1, lambda k, u=u: lambda: m_interleave(u))
+            add(u + 4.6, 0, 1, lambda k, u=u: lambda: m_quantise(u))
+            add(u + 5, 1, 2 * TILES, lambda k, u=u: lambda: feed_forward(u, k))
+            add(u + 5.25, 1, TILES, lambda k, u=u: lambda: relu_store(u, k))
+        add(1.5, 0, 1, lambda k: prepare_vectors)
+        add(1.5, 0.5, 2, lambda k: lambda: prepare_bias(k))
+        add(2, 1, 4, lambda k: lambda: prepare_ff1(k))
+        add(3.1, 0.3, 2, lambda k: lambda: quantise_ff1(k))
+        for key, order, run in sorted(atoms, key=lambda a: (a[0], a[1])):
+            run()

@@ -21,10 +21,54 @@ F = 1024
 BANK = 512
 EPS = 1e-5
 F32_MAX = 3.4028234663852886e38
-TILES = 2
-TOKENS = TILES * P
-PARTS = T // TOKENS
-UNITS = SEQS * PARTS
+CUTS = [[2, 2]] * SEQS
+RBUFS = 6
+PBUFS = 3
+GBUFS = 3
+RESBUFS = 8
+PST = 4
+ARS = True
+NEGG = True
+O = dict(A1=0.5, Q1=0.75, M1=1, SQ=1.25, NM=2.25, RS=2.25, RC=2.5, SM=2.6, N0=2.75, N1=0, B0=3, B1=0.75, I=4, I1=0, Q2=4.5, M2=5, R=5.5, ST=5.5, KB=3, KP=4)
+
+
+def BIASCOPY(nc):
+    return nc.scalar.copy
+
+
+def FF1COPY(nc, k):
+    return nc.vector.tensor_copy if k % 2 else nc.scalar.copy
+
+
+def AXV(u, k):
+    return False
+
+
+def NORM(u, j):
+    return "V"
+
+
+def AFF(u, c):
+    return "S"
+
+
+def INTN(u):
+    return 1
+
+
+def INTER(u, k):
+    return "V"
+
+
+def RELUN(u):
+    return 1
+
+
+def RELU(u, j, q):
+    return "S"
+
+PIECES = [(s, sum(CUTS[s][:i]) * P, CUTS[s][i]) for s in range(SEQS) for i in range(len(CUTS[s]))]
+UNITS = len(PIECES)
 
 FLOPS = 2 * SEQS * T * D * (D + F)
 
@@ -36,9 +80,9 @@ def tile_temporalatt_pb_t_kernel(tc, ax_cat, features, wout_w, ln_g, ln_b, ff1_w
         inputs = stack.enter_context(tc.tile_pool(name="inputs", bufs=1))
         work = stack.enter_context(tc.tile_pool(name="work", bufs=3))
         stats = stack.enter_context(tc.tile_pool(name="stats", bufs=6))
-        results = stack.enter_context(tc.tile_pool(name="results", bufs=4))
-        ps_t = stack.enter_context(tc.psum_pool(name="ps_t", bufs=4))
-        ps_mx = stack.enter_context(tc.psum_pool(name="ps_mx", bufs=4))
+        results = stack.enter_context(tc.tile_pool(name="results", bufs=RESBUFS))
+        ps_t = stack.enter_context(tc.psum_pool(name="ps_t", bufs=PST))
+        ps_mx = stack.enter_context(tc.psum_pool(name="ps_mx", bufs=8 - PST))
         stack.enter_context(tc.manual_schedule())
 
         ident_f32 = const.tile([P, P], F32)
@@ -48,7 +92,7 @@ def tile_temporalatt_pb_t_kernel(tc, ax_cat, features, wout_w, ln_g, ln_b, ff1_w
         eps = const.tile([P, 1], F32)
         nc.vector.memset(eps[:], EPS)
         warm = const.tile([P, 1], F32)
-        nc.scalar.activation(out=warm[:], in_=eps[:], func=ACT.Sqrt)
+        nc.scalar.activation(out=warm[:], in_=eps[:], func=ACT.Abs_reciprocal_sqrt if ARS else ACT.Sqrt)
         bias_row = const.tile([P, F], BF16)
         nc.vector.memset(bias_row[:], 0.0)
 
@@ -58,19 +102,24 @@ def tile_temporalatt_pb_t_kernel(tc, ax_cat, features, wout_w, ln_g, ln_b, ff1_w
         x_sb = {}
 
         def load_ax(u):
-            ax_tile = inputs.tile([P, TILES, D], BF16, name="ax%d" % u)
-            ax_view = ax_cat[u // PARTS].rearrange("(h p j) d -> h p j d", h=PARTS, j=TILES)
-            nc.sync.dma_start(out=ax_tile[:], in_=ax_view[u % PARTS])
+            s, at, tiles = PIECES[u]
+            ax_tile = inputs.tile([P, tiles, D], BF16, name="ax%d" % u)
+            nc.sync.dma_start(
+                out=ax_tile[:], in_=ax_cat[s, at : at + tiles * P, :].rearrange("(p j) d -> p j d", j=tiles)
+            )
             ax_sb[u] = ax_tile
 
         def load_x(u):
-            s = u // PARTS
-            x_tile = inputs.tile([P, TILES, D], BF16, name="x%d" % u)
-            x_view = features[s // NODES].rearrange("(h p j) n d -> h p j n d", h=PARTS, j=TILES)
-            nc.sync.dma_start(out=x_tile[:], in_=x_view[u % PARTS][:, :, s % NODES, :])
+            s, at, tiles = PIECES[u]
+            x_tile = inputs.tile([P, tiles, D], BF16, name="x%d" % u)
+            nc.sync.dma_start(
+                out=x_tile[:],
+                in_=features[s // NODES, at : at + tiles * P, s % NODES, :].rearrange("(p j) d -> p j d", j=tiles),
+            )
             x_sb[u] = x_tile
 
-        nc.sync.dma_start(out=wout_sb[:], in_=wout_view)
+        for h in range(2):
+            nc.sync.dma_start(out=wout_sb[:, 2 * h : 2 * h + 2, :], in_=wout_view[:, 2 * h : 2 * h + 2, :])
         load_ax(0)
         load_x(0)
         load_ax(1)
@@ -89,17 +138,17 @@ def tile_temporalatt_pb_t_kernel(tc, ax_cat, features, wout_w, ln_g, ln_b, ff1_w
             load_ax(u)
             load_x(u)
 
-        def transpose_pair(rows_sb, i, grouped, engine):
-            bank = ps_t.tile([P, 2, 2, P], F32, tag="t")
-            for r in range(2):
+        def transpose_pair(rows_sb, i, grouped, engine, count=2):
+            bank = ps_t.tile([P, count, 2, P], F32, tag="t")
+            for r in range(count):
                 words = rows_sb[:, i + r, :].bitcast(F32)
                 for w in range(2):
                     nc.tensor.transpose(bank[:, r, w, :], words[:, w::2], ident_f32[:])
             engine(
-                out=grouped[:, i * P : (i + 2) * P, :]
+                out=grouped[:, i * P : (i + count) * P, :]
                 .rearrange("p n c -> p (n c)")
                 .bitcast(F32)
-                .rearrange("p (i r w) -> p i r w", i=2, w=2),
+                .rearrange("p (i r w) -> p i r w", i=count, w=2),
                 in_=bank[:].rearrange("p i w r -> p i r w"),
             )
 
@@ -119,8 +168,9 @@ def tile_temporalatt_pb_t_kernel(tc, ax_cat, features, wout_w, ln_g, ln_b, ff1_w
         ff1_scales = [const.tile([P, BANK], U8, name="ff1_scales%d" % h, align_bytes=64) for h in range(2)]
 
         transpose_pair(wout_sb, 0, wout_grouped, nc.scalar.copy)
+        quantise(wout_grouped[:, : 2 * P, :], wout_codes[:, : 2 * P], wout_scales[:, : 2 * P])
         transpose_pair(wout_sb, 2, wout_grouped, nc.vector.tensor_copy)
-        quantise(wout_grouped[:], wout_codes[:], wout_scales[:])
+        quantise(wout_grouped[:, 2 * P :, :], wout_codes[:, 2 * P :], wout_scales[:, 2 * P :])
 
         ax_grouped = {}
         ax_codes = {}
@@ -136,27 +186,34 @@ def tile_temporalatt_pb_t_kernel(tc, ax_cat, features, wout_w, ln_g, ln_b, ff1_w
         m_codes = {}
         m_scales = {}
         result = {}
+        offset = {}
+
+        def tiles_of(u):
+            return PIECES[u][2]
 
         def ax_transpose(u, k):
+            tiles = tiles_of(u)
             if k == 0:
-                fresh_ax_grouped = work.tile([P, TOKENS, PACK], BF16, tag="ax_grouped", align_bytes=64)
+                fresh_ax_grouped = work.tile([P, tiles * P, PACK], BF16, tag="ax_grouped", align_bytes=64)
                 ax_grouped[u] = fresh_ax_grouped
-            transpose_pair(ax_sb[u], 2 * k, ax_grouped[u], nc.scalar.copy);
+            transpose_pair(ax_sb[u], 2 * k, ax_grouped[u], nc.vector.tensor_copy if AXV(u, k) else nc.scalar.copy, min(2, tiles - 2 * k))
 
         def ax_quantise(u):
-            fresh_ax_codes = work.tile([P, TOKENS], U32, tag="ax_codes", align_bytes=64)
+            tokens = tiles_of(u) * P
+            fresh_ax_codes = work.tile([P, tokens], U32, tag="ax_codes", align_bytes=64)
             ax_codes[u] = fresh_ax_codes
-            fresh_ax_scales = work.tile([P, TOKENS], U8, tag="ax_scales", align_bytes=64)
+            fresh_ax_scales = work.tile([P, tokens], U8, tag="ax_scales", align_bytes=64)
             ax_scales[u] = fresh_ax_scales
             quantise(ax_grouped[u][:], ax_codes[u][:], ax_scales[u][:])
 
         def project(u, j):
+            tiles = tiles_of(u)
             if j == 0:
-                fresh_residual = work.tile([P, TILES, D], F32, tag="r", bufs=6)
+                fresh_residual = work.tile([P, tiles, D], F32, tag="r", bufs=RBUFS)
                 residual[u] = fresh_residual
-                fresh_row_sum = stats.tile([P, TILES], F32, tag="sums")
+                fresh_row_sum = stats.tile([P, tiles], F32, tag="sums")
                 row_sum[u] = fresh_row_sum
-                fresh_sum_sq = stats.tile([P, TILES], F32, tag="sum_sq")
+                fresh_sum_sq = stats.tile([P, tiles], F32, tag="sum_sq")
                 sum_sq[u] = fresh_sum_sq
             y = ps_mx.tile([P, D], F32, tag="mx")
             nc.tensor.matmul_mx(
@@ -190,70 +247,113 @@ def tile_temporalatt_pb_t_kernel(tc, ax_cat, features, wout_w, ln_g, ln_b, ff1_w
             )
 
         def finish_statistics(u):
-            fresh_neg_mean = stats.tile([P, TILES], F32, tag="neg_mean")
-            neg_mean[u] = fresh_neg_mean
-            nc.gpsimd.tensor_scalar(
-                out=neg_mean[u][:], in0=row_sum[u][:], scalar1=-1.0 / D, scalar2=0.0, op0=ALU.mult, op1=ALU.add
-            )
-            root = stats.tile([P, TILES], F32, tag="std")
-            nc.scalar.activation(out=root[:], in_=sum_sq[u][:], func=ACT.Sqrt, bias=eps[:], scale=1.0 / D**3)
+            tiles = tiles_of(u)
+            root = stats.tile([P, tiles], F32, tag="std")
+            nc.scalar.activation(out=root[:], in_=sum_sq[u][:], func=ACT.Abs_reciprocal_sqrt if ARS else ACT.Sqrt, bias=eps[:], scale=1.0 / D**3)
             std[u] = root
+            if ARS:
+                rstd[u] = root
+
+        def negate_mean(u):
+            fresh_neg_mean = stats.tile([P, tiles_of(u)], F32, tag="neg_mean")
+            neg_mean[u] = fresh_neg_mean
+            if NEGG:
+                nc.gpsimd.tensor_scalar(out=neg_mean[u][:], in0=row_sum[u][:], scalar1=-1.0 / D, scalar2=0.0, op0=ALU.mult, op1=ALU.add)
+            else:
+                nc.scalar.activation(out=neg_mean[u][:], in_=row_sum[u][:], func=ACT.Copy, scale=-1.0 / D)
 
         def invert(u):
-            fresh_rstd = stats.tile([P, TILES], F32, tag="rstd")
+            if ARS:
+                return
+            fresh_rstd = stats.tile([P, tiles_of(u)], F32, tag="rstd")
             rstd[u] = fresh_rstd
             nc.vector.reciprocal(out=rstd[u][:], in_=std[u][:])
 
+        def scale_mean(u):
+            fresh_offset = stats.tile([P, tiles_of(u)], F32, tag="offset")
+            offset[u] = fresh_offset
+            for j in range(tiles_of(u)):
+                if NORM(u, j) == "S":
+                    nc.scalar.activation(out=offset[u][:, j : j + 1], in_=neg_mean[u][:, j : j + 1], func=ACT.Copy, scale=rstd[u][:, j : j + 1])
+
         def normalise(u, j):
-            nc.vector.tensor_scalar(
-                out=residual[u][:, j, :],
-                in0=residual[u][:, j, :],
-                scalar1=neg_mean[u][:, j : j + 1],
-                scalar2=rstd[u][:, j : j + 1],
-                op0=ALU.add,
-                op1=ALU.mult,
-            )
+            tile = residual[u][:, j, :]
+            if NORM(u, j) == "S":
+                nc.scalar.activation(
+                    out=tile, in_=tile, func=ACT.Identity, scale=rstd[u][:, j : j + 1], bias=offset[u][:, j : j + 1]
+                )
+            else:
+                (nc.vector if NORM(u, j) == "V" else nc.gpsimd).tensor_scalar(
+                    out=tile,
+                    in0=tile,
+                    scalar1=neg_mean[u][:, j : j + 1],
+                    scalar2=rstd[u][:, j : j + 1],
+                    op0=ALU.add,
+                    op1=ALU.mult,
+                )
 
         def m_transpose(u, k):
+            tiles = tiles_of(u)
+            tokens = tiles * P
             if k == 0:
-                fresh_m_planes = work.tile([P, PACK, TOKENS], BF16, tag="planes")
+                fresh_m_planes = work.tile([P, PACK, tokens], BF16, tag="planes", bufs=PBUFS)
                 m_planes[u] = fresh_m_planes
-            group = BANK // TOKENS
-            bank = ps_t.tile([P, group, TILES, P], F32, tag="t")
+            group = BANK // tokens
+            bank = ps_t.tile([P, group, tiles, P], F32, tag="t")
             for i in range(group):
                 c = k * group + i
-                for j in range(TILES):
+                for j in range(tiles):
                     nc.tensor.transpose(bank[:, i, j, :], residual[u][:, j, c * P : (c + 1) * P], ident_f32[:])
             for i in range(group):
                 c = k * group + i
-                nc.scalar.activation(
-                    out=m_planes[u][:, c, :],
-                    in_=bank[:, i, :, :].rearrange("p j t -> p (j t)"),
-                    func=ACT.Identity,
-                    bias=shift[:, c : c + 1],
-                    scale=gain[:, c : c + 1],
-                )
+                if AFF(u, c) == "S":
+                    nc.scalar.activation(
+                        out=m_planes[u][:, c, :],
+                        in_=bank[:, i, :, :].rearrange("p j t -> p (j t)"),
+                        func=ACT.Identity,
+                        bias=shift[:, c : c + 1],
+                        scale=gain[:, c : c + 1],
+                    )
+                else:
+                    nc.vector.tensor_scalar(
+                        out=m_planes[u][:, c, :],
+                        in0=bank[:, i, :, :].rearrange("p j t -> p (j t)"),
+                        scalar1=gain[:, c : c + 1],
+                        scalar2=shift[:, c : c + 1],
+                        op0=ALU.mult,
+                        op1=ALU.add,
+                    )
 
-        def m_interleave(u):
-            fresh_m_grouped = work.tile([P, TOKENS, PACK], BF16, tag="grouped_m", align_bytes=64)
-            m_grouped[u] = fresh_m_grouped
-            nc.vector.tensor_copy(
-                out=m_grouped[u][:].rearrange("p (w i) c -> p w c i", i=4),
-                in_=m_planes[u][:].rearrange("p c (w i) -> p w c i", i=4),
-            )
+        def m_interleave(u, k):
+            tokens = tiles_of(u) * P
+            n = INTN(u)
+            if k == 0:
+                fresh_m_grouped = work.tile([P, tokens, PACK], BF16, tag="grouped_m", bufs=GBUFS, align_bytes=64)
+                m_grouped[u] = fresh_m_grouped
+            a, b = k * tokens // n, (k + 1) * tokens // n
+            target = m_grouped[u][:, a:b, :].rearrange("p (w i) c -> p w c i", i=4)
+            source = m_planes[u][:, :, a:b].rearrange("p c (w i) -> p w c i", i=4)
+            if INTER(u, k) == "V":
+                nc.vector.tensor_copy(out=target, in_=source)
+            elif INTER(u, k) == "S":
+                nc.scalar.copy(out=target, in_=source)
+            else:
+                nc.gpsimd.tensor_scalar(out=target, in0=source, scalar1=1.0, scalar2=0.0, op0=ALU.mult, op1=ALU.add)
 
         def m_quantise(u):
-            fresh_m_codes = work.tile([P, TOKENS], U32, tag="m_codes", align_bytes=64)
+            tokens = tiles_of(u) * P
+            fresh_m_codes = work.tile([P, tokens], U32, tag="m_codes", align_bytes=64)
             m_codes[u] = fresh_m_codes
-            fresh_m_scales = work.tile([P, TOKENS], U8, tag="m_scales", align_bytes=64)
+            fresh_m_scales = work.tile([P, tokens], U8, tag="m_scales", align_bytes=64)
             m_scales[u] = fresh_m_scales
             quantise(m_grouped[u][:], m_codes[u][:], m_scales[u][:])
 
         def feed_forward(u, k):
             j, h = divmod(k, 2)
-            if k == 0:
-                fresh_result = results.tile([P, TILES, F], F32, tag="result")
-                result[u] = fresh_result
+            tiles = tiles_of(u)
+            if h == 0:
+                fresh_result = results.tile([P, F], F32, tag="result")
+                result[u, j] = fresh_result
             acc = ps_mx.tile([P, BANK], F32, tag="mx")
             nc.tensor.matmul_mx(
                 out=acc[:],
@@ -265,23 +365,33 @@ def tile_temporalatt_pb_t_kernel(tc, ax_cat, features, wout_w, ln_g, ln_b, ff1_w
                 stop=True,
             )
             nc.vector.tensor_tensor(
-                out=result[u][:, j, h * BANK : (h + 1) * BANK],
+                out=result[u, j][:, h * BANK : (h + 1) * BANK],
                 in0=acc[:],
                 in1=bias_all[:, h * BANK : (h + 1) * BANK],
                 op=ALU.add,
             )
 
-        def relu_store(u, j):
-            tile = result[u][:, j, :]
-            which = ["S","S","S","S"][(u * TILES + j) % 4]
+        def relu(u, k):
+            n = RELUN(u)
+            j, q = divmod(k, n)
+            tile = result[u, j][:, q * F // n : (q + 1) * F // n]
+            which = RELU(u, j, q)
             if which == "S":
                 nc.scalar.activation(out=tile, in_=tile, func=ACT.Relu)
             elif which == "V":
                 nc.vector.tensor_scalar_max(out=tile, in0=tile, scalar1=0.0)
             else:
                 nc.gpsimd.tensor_scalar(out=tile, in0=tile, scalar1=F32_MAX, scalar2=0.0, op0=ALU.min, op1=ALU.max)
-            out_view = out[u // PARTS].rearrange("(h p j) f -> h p j f", h=PARTS, j=TILES)[u % PARTS]
-            nc.sync.dma_start(out=out_view[:, j, :], in_=tile)
+
+        def store(u, k):
+            s, at, tiles = PIECES[u]
+            n = RELUN(u)
+            j, q = divmod(k, n)
+            cols = slice(q * F // n, (q + 1) * F // n)
+            nc.sync.dma_start(
+                out=out[s, at : at + tiles * P, :].rearrange("(p j) f -> p j f", j=tiles)[:, j, cols],
+                in_=result[u, j][:, cols],
+            )
 
         def prepare_vectors():
             nc.vector.tensor_copy(out=gain[:], in_=gain_rows[:])
@@ -292,37 +402,48 @@ def tile_temporalatt_pb_t_kernel(tc, ax_cat, features, wout_w, ln_g, ln_b, ff1_w
             nc.tensor.matmul(
                 out=bias_bank[:], lhsT=ones[:], rhs=bias_row[:, h * BANK : (h + 1) * BANK], start=True, stop=True
             )
-            nc.scalar.copy(out=bias_all[:, h * BANK : (h + 1) * BANK], in_=bias_bank[:])
+            BIASCOPY(nc)(out=bias_all[:, h * BANK : (h + 1) * BANK], in_=bias_bank[:])
 
         def prepare_ff1(k):
             h, i = divmod(k, 2)
-            transpose_pair(ff1_sb[:, 4 * h : 4 * h + 4, :], 2 * i, ff1_grouped[h], nc.scalar.copy if i == 0 else nc.vector.tensor_copy)
+            transpose_pair(ff1_sb[:, 4 * h : 4 * h + 4, :], 2 * i, ff1_grouped[h], FF1COPY(nc, k))
 
         def quantise_ff1(h):
             quantise(ff1_grouped[h][:], ff1_codes[h][:], ff1_scales[h][:])
 
         atoms = []
+        START = [sum(p[2] for p in PIECES[:u]) for u in range(UNITS + 1)]
 
-        def add(at, spread, n, make):
+        def add(u, at, spread, n, make):
+            tiles = tiles_of(u)
+            for k in range(n):
+                atoms.append((START[u] + tiles * (at + spread * (k + 0.5) / n), len(atoms), make(k)))
+
+        def add_at(at, spread, n, make):
             for k in range(n):
                 atoms.append((at + spread * (k + 0.5) / n, len(atoms), make(k)))
 
         for u in range(UNITS):
-            add(u + 0, 0.5, TILES // 2, lambda k, u=u: lambda: ax_transpose(u, k))
-            add(u + 0.75, 0, 1, lambda k, u=u: lambda: ax_quantise(u))
-            add(u + 1, 1, TILES, lambda k, u=u: lambda: project(u, k))
-            add(u + 1.3, 1, TILES, lambda k, u=u: lambda: square(u, k))
-            add(u + 2.35, 0, 1, lambda k, u=u: lambda: finish_statistics(u))
-            add(u + 2.7, 0, 1, lambda k, u=u: lambda: invert(u))
-            add(u + 2.75, 0.5, TILES, lambda k, u=u: lambda: normalise(u, k))
-            add(u + 3.3, 0.7, TILES, lambda k, u=u: lambda: m_transpose(u, k))
-            add(u + 4.2, 0, 1, lambda k, u=u: lambda: m_interleave(u))
-            add(u + 4.6, 0, 1, lambda k, u=u: lambda: m_quantise(u))
-            add(u + 5, 1, 2 * TILES, lambda k, u=u: lambda: feed_forward(u, k))
-            add(u + 5.25, 1, TILES, lambda k, u=u: lambda: relu_store(u, k))
-        add(1.5, 0, 1, lambda k: prepare_vectors)
-        add(1.5, 0.5, 2, lambda k: lambda: prepare_bias(k))
-        add(2, 1, 4, lambda k: lambda: prepare_ff1(k))
-        add(3.1, 0.3, 2, lambda k: lambda: quantise_ff1(k))
+            n = tiles_of(u)
+            add(u, 0, O["A1"], (n + 1) // 2, lambda k, u=u: lambda: ax_transpose(u, k))
+            add(u, O["Q1"], 0, 1, lambda k, u=u: lambda: ax_quantise(u))
+            add(u, O["M1"], 1, n, lambda k, u=u: lambda: project(u, k))
+            add(u, O["SQ"], 1, n, lambda k, u=u: lambda: square(u, k))
+            add(u, O["NM"], 0, 1, lambda k, u=u: lambda: negate_mean(u))
+            add(u, O["RS"], 0, 1, lambda k, u=u: lambda: finish_statistics(u))
+            add(u, O["RC"], 0, 1, lambda k, u=u: lambda: invert(u))
+            if any(NORM(u, j) == "S" for j in range(n)):
+                add(u, O["SM"], 0, 1, lambda k, u=u: lambda: scale_mean(u))
+            add(u, O["N0"], O["N1"], n, lambda k, u=u: lambda: normalise(u, k))
+            add(u, O["B0"], O["B1"], n, lambda k, u=u: lambda: m_transpose(u, k))
+            add(u, O["I"], O["I1"], INTN(u), lambda k, u=u: lambda: m_interleave(u, k))
+            add(u, O["Q2"], 0, 1, lambda k, u=u: lambda: m_quantise(u))
+            add(u, O["M2"], 1, 2 * n, lambda k, u=u: lambda: feed_forward(u, k))
+            add(u, O["R"], 1, n * RELUN(u), lambda k, u=u: lambda: relu(u, k))
+            add(u, O["ST"], 1, n * RELUN(u), lambda k, u=u: lambda: store(u, k))
+        add_at(O["KB"], 0, 1, lambda k: prepare_vectors)
+        add_at(O["KB"], 1, 2, lambda k: lambda: prepare_bias(k))
+        add_at(O["KP"], 2, 4, lambda k: lambda: prepare_ff1(k))
+        add_at(O["KP"] + 2.2, 0.6, 2, lambda k: lambda: quantise_ff1(k))
         for key, order, run in sorted(atoms, key=lambda a: (a[0], a[1])):
             run()

@@ -29,7 +29,7 @@ RESBUFS = 8
 PST = 4
 ARS = True
 NEGG = True
-O = dict(A1=0.5, Q1=0.75, M1=1, SQ=1.25, NM=2.25, RS=2.25, RC=2.5, SM=2.6, N0=2.75, N1=0, B0=3, B1=0.75, I=4, I1=0, Q2=4.5, M2=5, R=5.5, ST=5.5, KB=3, KP=4)
+O = dict(XT=0, XC=0.25, Q1=1, PM=1.25, PM1=1, T=1.5, SQ=1.75, RS=2.75, RC=2.75, N0=3, N1=0.25, MT=3.75, MT1=0.5, AF=3.75, AF1=0.5, I=4.5, Q2=5, FM=5.25, FM1=1, B=5.5, R=6, KB=3, KP=4)
 
 
 def BIASCOPY(nc):
@@ -138,12 +138,23 @@ def tile_temporalatt_pb_t_kernel(tc, ax_cat, features, wout_w, ln_g, ln_b, ff1_w
             load_ax(u)
             load_x(u)
 
+        held = {"t": 0, "mx": 0}
+
         def transpose_pair(rows_sb, i, grouped, engine, count=2):
+            empty_pair(fill_pair(rows_sb, i, count), i, grouped, engine, count)
+
+        def fill_pair(rows_sb, i, count):
+            held["t"] += 1
+            assert held["t"] <= PST
             bank = ps_t.tile([P, count, 2, P], F32, tag="t")
             for r in range(count):
                 words = rows_sb[:, i + r, :].bitcast(F32)
                 for w in range(2):
                     nc.tensor.transpose(bank[:, r, w, :], words[:, w::2], ident_f32[:])
+            return bank
+
+        def empty_pair(bank, i, grouped, engine, count):
+            held["t"] -= 1
             engine(
                 out=grouped[:, i * P : (i + count) * P, :]
                 .rearrange("p n c -> p (n c)")
@@ -187,6 +198,10 @@ def tile_temporalatt_pb_t_kernel(tc, ax_cat, features, wout_w, ln_g, ln_b, ff1_w
         m_scales = {}
         result = {}
         offset = {}
+        ax_bank = {}
+        m_bank = {}
+        y_bank = {}
+        acc_bank = {}
 
         def tiles_of(u):
             return PIECES[u][2]
@@ -196,7 +211,12 @@ def tile_temporalatt_pb_t_kernel(tc, ax_cat, features, wout_w, ln_g, ln_b, ff1_w
             if k == 0:
                 fresh_ax_grouped = work.tile([P, tiles * P, PACK], BF16, tag="ax_grouped", align_bytes=64)
                 ax_grouped[u] = fresh_ax_grouped
-            transpose_pair(ax_sb[u], 2 * k, ax_grouped[u], nc.vector.tensor_copy if AXV(u, k) else nc.scalar.copy, min(2, tiles - 2 * k))
+            ax_bank[u, k] = fill_pair(ax_sb[u], 2 * k, min(2, tiles - 2 * k))
+
+        def ax_copy(u, k):
+            empty_pair(
+                ax_bank[u, k], 2 * k, ax_grouped[u], nc.vector.tensor_copy if AXV(u, k) else nc.scalar.copy, min(2, tiles_of(u) - 2 * k)
+            )
 
         def ax_quantise(u):
             tokens = tiles_of(u) * P
@@ -207,14 +227,8 @@ def tile_temporalatt_pb_t_kernel(tc, ax_cat, features, wout_w, ln_g, ln_b, ff1_w
             quantise(ax_grouped[u][:], ax_codes[u][:], ax_scales[u][:])
 
         def project(u, j):
-            tiles = tiles_of(u)
-            if j == 0:
-                fresh_residual = work.tile([P, tiles, D], F32, tag="r", bufs=RBUFS)
-                residual[u] = fresh_residual
-                fresh_row_sum = stats.tile([P, tiles], F32, tag="sums")
-                row_sum[u] = fresh_row_sum
-                fresh_sum_sq = stats.tile([P, tiles], F32, tag="sum_sq")
-                sum_sq[u] = fresh_sum_sq
+            held["mx"] += 1
+            assert held["mx"] <= 8 - PST
             y = ps_mx.tile([P, D], F32, tag="mx")
             nc.tensor.matmul_mx(
                 out=y[:],
@@ -225,6 +239,19 @@ def tile_temporalatt_pb_t_kernel(tc, ax_cat, features, wout_w, ln_g, ln_b, ff1_w
                 start=True,
                 stop=True,
             )
+            y_bank[u, j] = y
+
+        def add_residual(u, j):
+            held["mx"] -= 1
+            tiles = tiles_of(u)
+            y = y_bank[u, j]
+            if j == 0:
+                fresh_residual = work.tile([P, tiles, D], F32, tag="r", bufs=RBUFS)
+                residual[u] = fresh_residual
+                fresh_row_sum = stats.tile([P, tiles], F32, tag="sums")
+                row_sum[u] = fresh_row_sum
+                fresh_sum_sq = stats.tile([P, tiles], F32, tag="sum_sq")
+                sum_sq[u] = fresh_sum_sq
             nc.vector.scalar_tensor_tensor(
                 out=residual[u][:, j, :].rearrange("p (t i) -> p t i", t=PACK),
                 in0=y[:].rearrange("p (t i) -> p t i", t=PACK),
@@ -299,11 +326,20 @@ def tile_temporalatt_pb_t_kernel(tc, ax_cat, features, wout_w, ln_g, ln_b, ff1_w
                 fresh_m_planes = work.tile([P, PACK, tokens], BF16, tag="planes", bufs=PBUFS)
                 m_planes[u] = fresh_m_planes
             group = BANK // tokens
+            held["t"] += 1
+            assert held["t"] <= PST
             bank = ps_t.tile([P, group, tiles, P], F32, tag="t")
+            m_bank[u, k] = bank
             for i in range(group):
                 c = k * group + i
                 for j in range(tiles):
                     nc.tensor.transpose(bank[:, i, j, :], residual[u][:, j, c * P : (c + 1) * P], ident_f32[:])
+
+        def affine(u, k):
+            held["t"] -= 1
+            tiles = tiles_of(u)
+            group = BANK // (tiles * P)
+            bank = m_bank[u, k]
             for i in range(group):
                 c = k * group + i
                 if AFF(u, c) == "S":
@@ -350,10 +386,8 @@ def tile_temporalatt_pb_t_kernel(tc, ax_cat, features, wout_w, ln_g, ln_b, ff1_w
 
         def feed_forward(u, k):
             j, h = divmod(k, 2)
-            tiles = tiles_of(u)
-            if h == 0:
-                fresh_result = results.tile([P, F], F32, tag="result")
-                result[u, j] = fresh_result
+            held["mx"] += 1
+            assert held["mx"] <= 8 - PST
             acc = ps_mx.tile([P, BANK], F32, tag="mx")
             nc.tensor.matmul_mx(
                 out=acc[:],
@@ -364,6 +398,15 @@ def tile_temporalatt_pb_t_kernel(tc, ax_cat, features, wout_w, ln_g, ln_b, ff1_w
                 start=True,
                 stop=True,
             )
+            acc_bank[u, k] = acc
+
+        def add_bias(u, k):
+            held["mx"] -= 1
+            j, h = divmod(k, 2)
+            acc = acc_bank[u, k]
+            if h == 0:
+                fresh_result = results.tile([P, F], F32, tag="result")
+                result[u, j] = fresh_result
             nc.vector.tensor_tensor(
                 out=result[u, j][:, h * BANK : (h + 1) * BANK],
                 in0=acc[:],
@@ -398,6 +441,7 @@ def tile_temporalatt_pb_t_kernel(tc, ax_cat, features, wout_w, ln_g, ln_b, ff1_w
             nc.vector.tensor_copy(out=shift[:], in_=shift_rows[:])
 
         def prepare_bias(h):
+            assert held["mx"] < 8 - PST
             bias_bank = ps_mx.tile([P, BANK], F32, tag="mx")
             nc.tensor.matmul(
                 out=bias_bank[:], lhsT=ones[:], rhs=bias_row[:, h * BANK : (h + 1) * BANK], start=True, stop=True
@@ -425,22 +469,28 @@ def tile_temporalatt_pb_t_kernel(tc, ax_cat, features, wout_w, ln_g, ln_b, ff1_w
 
         for u in range(UNITS):
             n = tiles_of(u)
-            add(u, 0, O["A1"], (n + 1) // 2, lambda k, u=u: lambda: ax_transpose(u, k))
+            banks = n * D // BANK
+            add(u, O["XT"], 0.5, (n + 1) // 2, lambda k, u=u: lambda: ax_transpose(u, k))
+            add(u, O["XC"], 0.5, (n + 1) // 2, lambda k, u=u: lambda: ax_copy(u, k))
             add(u, O["Q1"], 0, 1, lambda k, u=u: lambda: ax_quantise(u))
-            add(u, O["M1"], 1, n, lambda k, u=u: lambda: project(u, k))
+            add(u, O["PM"], O["PM1"], n, lambda k, u=u: lambda: project(u, k))
+            add(u, O["T"], 1, n, lambda k, u=u: lambda: add_residual(u, k))
             add(u, O["SQ"], 1, n, lambda k, u=u: lambda: square(u, k))
-            add(u, O["NM"], 0, 1, lambda k, u=u: lambda: negate_mean(u))
+            add(u, O["RS"], 0, 1, lambda k, u=u: lambda: negate_mean(u))
             add(u, O["RS"], 0, 1, lambda k, u=u: lambda: finish_statistics(u))
-            add(u, O["RC"], 0, 1, lambda k, u=u: lambda: invert(u))
+            if not ARS:
+                add(u, O["RC"], 0, 1, lambda k, u=u: lambda: invert(u))
             if any(NORM(u, j) == "S" for j in range(n)):
-                add(u, O["SM"], 0, 1, lambda k, u=u: lambda: scale_mean(u))
+                add(u, O["N0"], 0, 1, lambda k, u=u: lambda: scale_mean(u))
             add(u, O["N0"], O["N1"], n, lambda k, u=u: lambda: normalise(u, k))
-            add(u, O["B0"], O["B1"], n, lambda k, u=u: lambda: m_transpose(u, k))
-            add(u, O["I"], O["I1"], INTN(u), lambda k, u=u: lambda: m_interleave(u, k))
+            add(u, O["MT"], O["MT1"], banks, lambda k, u=u: lambda: m_transpose(u, k))
+            add(u, O["AF"], O["AF1"], banks, lambda k, u=u: lambda: affine(u, k))
+            add(u, O["I"], 0, 1, lambda k, u=u: lambda: m_interleave(u, k))
             add(u, O["Q2"], 0, 1, lambda k, u=u: lambda: m_quantise(u))
-            add(u, O["M2"], 1, 2 * n, lambda k, u=u: lambda: feed_forward(u, k))
+            add(u, O["FM"], O["FM1"], 2 * n, lambda k, u=u: lambda: feed_forward(u, k))
+            add(u, O["B"], 1, 2 * n, lambda k, u=u: lambda: add_bias(u, k))
             add(u, O["R"], 1, n * RELUN(u), lambda k, u=u: lambda: relu(u, k))
-            add(u, O["ST"], 1, n * RELUN(u), lambda k, u=u: lambda: store(u, k))
+            add(u, O["R"], 1, n * RELUN(u), lambda k, u=u: lambda: store(u, k))
         add_at(O["KB"], 0, 1, lambda k: prepare_vectors)
         add_at(O["KB"], 1, 2, lambda k: lambda: prepare_bias(k))
         add_at(O["KP"], 2, 4, lambda k: lambda: prepare_ff1(k))

@@ -29,7 +29,7 @@ RESBUFS = 8
 PST = 4
 ARS = True
 NEGG = True
-O = dict(XT=0, XC=0.25, Q1=1, PM=1.25, PM1=1, T=1.5, SQ=1.75, RS=2.75, RC=2.75, N0=3, N1=0.25, MT=3.75, MT1=0.5, AF=3.75, AF1=0.5, I=4.5, Q2=5, FM=5.25, FM1=1, B=5.5, R=6, KB=3, KP=4)
+O = dict(XT=0, XC=0.25, Q1=1, PM=1.25, PM1=1, T=1.5, SQ=1.75, RS=2.6, RC=2.75, N0=2.75, N1=0.25, MT=3.75, MT1=0.25, AF=3.75, AF1=0.5, I=4.5, Q2=5, FM=5.25, FM1=1, B=5.5, R=6, KB=3, KP=6)
 
 
 def BIASCOPY(nc):
@@ -41,11 +41,11 @@ def FF1COPY(nc, k):
 
 
 def AXV(u, k):
-    return False
+    return u % 4 == 1
 
 
 def NORM(u, j):
-    return "V"
+    return "G"
 
 
 def AFF(u, c):

@@ -28,8 +28,8 @@ GBUFS = 3
 RESBUFS = 8
 PST = 4
 ARS = True
-NEGG = True
-O = dict(XT=0, XC=0.25, Q1=1, PM=1.25, PM1=1, T=1.5, SQ=1.75, RS=2.6, RC=2.75, N0=2.75, N1=0.25, MT=3.75, MT1=0.25, AF=3.75, AF1=0.5, I=4.5, Q2=5, FM=5.25, FM1=1, B=5.5, R=6, KB=3, KP=6)
+NEGG = False
+O = dict(XT=0, XC=0.25, Q1=1, PM=1.25, PM1=1, T=1.5, SQ=1.75, RS=2.6, RC=2.75, N0=2.75, N1=0.25, MT=3.75, MT1=0.25, AF=3.75, AF1=0.5, I=4.5, Q2=5, FM=5.25, FM1=1, B=5.5, R=6, KB=4, KP=6)
 
 
 def BIASCOPY(nc):
@@ -41,7 +41,7 @@ def FF1COPY(nc, k):
 
 
 def AXV(u, k):
-    return u % 4 == 1
+    return True
 
 
 def NORM(u, j):
@@ -57,7 +57,7 @@ def INTN(u):
 
 
 def INTER(u, k):
-    return "V"
+    return "G"
 
 
 def RELUN(u):
@@ -485,7 +485,7 @@ def tile_temporalatt_pb_t_kernel(tc, ax_cat, features, wout_w, ln_g, ln_b, ff1_w
             add(u, O["N0"], O["N1"], n, lambda k, u=u: lambda: normalise(u, k))
             add(u, O["MT"], O["MT1"], banks, lambda k, u=u: lambda: m_transpose(u, k))
             add(u, O["AF"], O["AF1"], banks, lambda k, u=u: lambda: affine(u, k))
-            add(u, O["I"], 0, 1, lambda k, u=u: lambda: m_interleave(u, k))
+            add(u, O["I"], 0, INTN(u), lambda k, u=u: lambda: m_interleave(u, k))
             add(u, O["Q2"], 0, 1, lambda k, u=u: lambda: m_quantise(u))
             add(u, O["FM"], O["FM1"], 2 * n, lambda k, u=u: lambda: feed_forward(u, k))
             add(u, O["B"], 1, 2 * n, lambda k, u=u: lambda: add_bias(u, k))

@@ -49,7 +49,7 @@ def NORM(u, j):
 
 
 def AFF(u, c):
-    return "S"
+    return "V" if c == 1 and u % 2 else "S"
 
 
 def INTN(u):
@@ -61,7 +61,7 @@ def INTER(u, k):
 
 
 def RELUN(u):
-    return 1
+    return 2 if u >= 12 else 1
 
 
 def RELU(u, j, q):

from contextlib import ExitStack

import concourse.mybir as mybir
from concourse.masks import make_identity

F32 = mybir.dt.float32
BF16 = mybir.dt.bfloat16
U32 = mybir.dt.uint32
U8 = mybir.dt.uint8
FP8X4 = mybir.dt.float8_e4m3fn_x4
ALU = mybir.AluOpType
ACT = mybir.ActivationFunctionType

P = 128
PACK = 4
BATCH, NODES = 2, 4
SEQS = BATCH * NODES
T = 512
D = 512
F = 1024
BANK = 512
EPS = 1e-5
F32_MAX = 3.4028234663852886e38
CUTS = [[2, 2]] * SEQS
RBUFS = 6
PBUFS = 3
GBUFS = 3
RESBUFS = 8
PST = 4
ARS = True
NEGG = False
O = dict(XT=0, XC=0.25, Q1=1, PM=1.25, PM1=1, T=1.5, SQ=1.75, RS=2.6, RC=2.75, N0=2.75, N1=0.25, MT=3.75, MT1=0.25, AF=3.75, AF1=0.5, I=4.5, Q2=5, FM=5.25, FM1=1, B=5.5, R=6, KB=4, KP=6)


def BIASCOPY(nc):
    return nc.scalar.copy


def FF1COPY(nc, k):
    return nc.vector.tensor_copy if k % 2 else nc.scalar.copy


def AXV(u, k):
    return True


def NORM(u, j):
    return "G"


def AFF(u, c):
    return "V" if c == 1 and u % 2 else "S"


def INTN(u):
    return 1


def INTER(u, k):
    return "G"


def RELUN(u):
    return 2 if u >= 12 else 1


def RELU(u, j, q):
    return "S"

PIECES = [(s, sum(CUTS[s][:i]) * P, CUTS[s][i]) for s in range(SEQS) for i in range(len(CUTS[s]))]
UNITS = len(PIECES)

FLOPS = 2 * SEQS * T * D * (D + F)


def tile_temporalatt_pb_t_kernel(tc, ax_cat, features, wout_w, ln_g, ln_b, ff1_w, ff1_b, out):
    nc = tc.nc
    with ExitStack() as stack:
        const = stack.enter_context(tc.tile_pool(name="const", bufs=1))
        inputs = stack.enter_context(tc.tile_pool(name="inputs", bufs=1))
        work = stack.enter_context(tc.tile_pool(name="work", bufs=3))
        stats = stack.enter_context(tc.tile_pool(name="stats", bufs=6))
        results = stack.enter_context(tc.tile_pool(name="results", bufs=RESBUFS))
        ps_t = stack.enter_context(tc.psum_pool(name="ps_t", bufs=PST))
        ps_mx = stack.enter_context(tc.psum_pool(name="ps_mx", bufs=8 - PST))
        stack.enter_context(tc.manual_schedule())

        ident_f32 = const.tile([P, P], F32)
        make_identity(nc, ident_f32[:])
        ones = const.tile([P, P], BF16)
        nc.vector.memset(ones[:], 1.0)
        eps = const.tile([P, 1], F32)
        nc.vector.memset(eps[:], EPS)
        warm = const.tile([P, 1], F32)
        nc.scalar.activation(out=warm[:], in_=eps[:], func=ACT.Abs_reciprocal_sqrt if ARS else ACT.Sqrt)
        bias_row = const.tile([P, F], BF16)
        nc.vector.memset(bias_row[:], 0.0)

        wout_sb = const.tile([P, PACK, D], BF16)
        wout_view = wout_w.rearrange("(p o) k -> p o k", o=PACK)
        ax_sb = {}
        x_sb = {}

        def load_ax(u):
            s, at, tiles = PIECES[u]
            ax_tile = inputs.tile([P, tiles, D], BF16, name="ax%d" % u)
            nc.sync.dma_start(
                out=ax_tile[:], in_=ax_cat[s, at : at + tiles * P, :].rearrange("(p j) d -> p j d", j=tiles)
            )
            ax_sb[u] = ax_tile

        def load_x(u):
            s, at, tiles = PIECES[u]
            x_tile = inputs.tile([P, tiles, D], BF16, name="x%d" % u)
            nc.sync.dma_start(
                out=x_tile[:],
                in_=features[s // NODES, at : at + tiles * P, s % NODES, :].rearrange("(p j) d -> p j d", j=tiles),
            )
            x_sb[u] = x_tile

        for h in range(2):
            nc.sync.dma_start(out=wout_sb[:, 2 * h : 2 * h + 2, :], in_=wout_view[:, 2 * h : 2 * h + 2, :])
        load_ax(0)
        load_x(0)
        load_ax(1)
        gain_rows = const.tile([P, PACK], BF16)
        nc.sync.dma_start(out=gain_rows[:], in_=ln_g.rearrange("(p c) -> p c", c=PACK))
        shift_rows = const.tile([P, PACK], BF16)
        nc.sync.dma_start(out=shift_rows[:], in_=ln_b.rearrange("(p c) -> p c", c=PACK))
        nc.sync.dma_start(out=bias_row[0:1, :], in_=ff1_b.rearrange("(o f) -> o f", o=1))
        load_x(1)
        ff1_sb = const.tile([P, F // P, D], BF16)
        for q in range(2):
            nc.sync.dma_start(
                out=ff1_sb[:, 4 * q : 4 * q + 4, :], in_=ff1_w[512 * q : 512 * (q + 1), :].rearrange("(o p) k -> p o k", p=P)
            )
        for u in range(2, UNITS):
            load_ax(u)
            load_x(u)

        held = {"t": 0, "mx": 0}

        def transpose_pair(rows_sb, i, grouped, engine, count=2):
            empty_pair(fill_pair(rows_sb, i, count), i, grouped, engine, count)

        def fill_pair(rows_sb, i, count):
            held["t"] += 1
            assert held["t"] <= PST
            bank = ps_t.tile([P, count, 2, P], F32, tag="t")
            for r in range(count):
                words = rows_sb[:, i + r, :].bitcast(F32)
                for w in range(2):
                    nc.tensor.transpose(bank[:, r, w, :], words[:, w::2], ident_f32[:])
            return bank

        def empty_pair(bank, i, grouped, engine, count):
            held["t"] -= 1
            engine(
                out=grouped[:, i * P : (i + count) * P, :]
                .rearrange("p n c -> p (n c)")
                .bitcast(F32)
                .rearrange("p (i r w) -> p i r w", i=count, w=2),
                in_=bank[:].rearrange("p i w r -> p i r w"),
            )

        def quantise(grouped, codes, scales):
            nc.vector.quantize_mx(
                out=codes.bitcast(FP8X4), scales=scales, in_=grouped.rearrange("p r t -> p (r t)")
            )

        wout_grouped = const.tile([P, D, PACK], BF16, align_bytes=64)
        wout_codes = const.tile([P, D], U32, align_bytes=64)
        wout_scales = const.tile([P, D], U8, align_bytes=64)
        gain = const.tile([P, PACK], F32)
        shift = const.tile([P, PACK], F32)
        bias_all = const.tile([P, F], F32)
        ff1_grouped = [const.tile([P, BANK, PACK], BF16, name="ff1_grouped%d" % h, align_bytes=64) for h in range(2)]
        ff1_codes = [const.tile([P, BANK], U32, name="ff1_codes%d" % h, align_bytes=64) for h in range(2)]
        ff1_scales = [const.tile([P, BANK], U8, name="ff1_scales%d" % h, align_bytes=64) for h in range(2)]

        transpose_pair(wout_sb, 0, wout_grouped, nc.scalar.copy)
        quantise(wout_grouped[:, : 2 * P, :], wout_codes[:, : 2 * P], wout_scales[:, : 2 * P])
        transpose_pair(wout_sb, 2, wout_grouped, nc.vector.tensor_copy)
        quantise(wout_grouped[:, 2 * P :, :], wout_codes[:, 2 * P :], wout_scales[:, 2 * P :])

        ax_grouped = {}
        ax_codes = {}
        ax_scales = {}
        residual = {}
        row_sum = {}
        sum_sq = {}
        neg_mean = {}
        std = {}
        rstd = {}
        m_planes = {}
        m_grouped = {}
        m_codes = {}
        m_scales = {}
        result = {}
        offset = {}
        ax_bank = {}
        m_bank = {}
        y_bank = {}
        acc_bank = {}

        def tiles_of(u):
            return PIECES[u][2]

        def ax_transpose(u, k):
            tiles = tiles_of(u)
            if k == 0:
                fresh_ax_grouped = work.tile([P, tiles * P, PACK], BF16, tag="ax_grouped", align_bytes=64)
                ax_grouped[u] = fresh_ax_grouped
            ax_bank[u, k] = fill_pair(ax_sb[u], 2 * k, min(2, tiles - 2 * k))

        def ax_copy(u, k):
            empty_pair(
                ax_bank[u, k], 2 * k, ax_grouped[u], nc.vector.tensor_copy if AXV(u, k) else nc.scalar.copy, min(2, tiles_of(u) - 2 * k)
            )

        def ax_quantise(u):
            tokens = tiles_of(u) * P
            fresh_ax_codes = work.tile([P, tokens], U32, tag="ax_codes", align_bytes=64)
            ax_codes[u] = fresh_ax_codes
            fresh_ax_scales = work.tile([P, tokens], U8, tag="ax_scales", align_bytes=64)
            ax_scales[u] = fresh_ax_scales
            quantise(ax_grouped[u][:], ax_codes[u][:], ax_scales[u][:])

        def project(u, j):
            held["mx"] += 1
            assert held["mx"] <= 8 - PST
            y = ps_mx.tile([P, D], F32, tag="mx")
            nc.tensor.matmul_mx(
                out=y[:],
                lhsT=ax_codes[u][:, j * P : (j + 1) * P].bitcast(FP8X4),
                lhsT_scale=ax_scales[u][:, j * P : (j + 1) * P],
                rhs=wout_codes[:].bitcast(FP8X4),
                rhs_scale=wout_scales[:],
                start=True,
                stop=True,
            )
            y_bank[u, j] = y

        def add_residual(u, j):
            held["mx"] -= 1
            tiles = tiles_of(u)
            y = y_bank[u, j]
            if j == 0:
                fresh_residual = work.tile([P, tiles, D], F32, tag="r", bufs=RBUFS)
                residual[u] = fresh_residual
                fresh_row_sum = stats.tile([P, tiles], F32, tag="sums")
                row_sum[u] = fresh_row_sum
                fresh_sum_sq = stats.tile([P, tiles], F32, tag="sum_sq")
                sum_sq[u] = fresh_sum_sq
            nc.vector.scalar_tensor_tensor(
                out=residual[u][:, j, :].rearrange("p (t i) -> p t i", t=PACK),
                in0=y[:].rearrange("p (t i) -> p t i", t=PACK),
                scalar=1.0,
                in1=x_sb[u][:, j, :].rearrange("p (i t) -> p t i", t=PACK),
                op0=ALU.mult,
                op1=ALU.add,
                accum_out=row_sum[u][:, j : j + 1],
            )

        def square(u, j):
            squares = work.tile([P, D], BF16, tag="squares", bufs=2)
            nc.scalar.activation(
                out=squares[:],
                in_=residual[u][:, j, :],
                func=ACT.Square,
                bias=row_sum[u][:, j : j + 1],
                scale=-float(D),
                accum_out=sum_sq[u][:, j : j + 1],
            )

        def finish_statistics(u):
            tiles = tiles_of(u)
            root = stats.tile([P, tiles], F32, tag="std")
            nc.scalar.activation(out=root[:], in_=sum_sq[u][:], func=ACT.Abs_reciprocal_sqrt if ARS else ACT.Sqrt, bias=eps[:], scale=1.0 / D**3)
            std[u] = root
            if ARS:
                rstd[u] = root

        def negate_mean(u):
            fresh_neg_mean = stats.tile([P, tiles_of(u)], F32, tag="neg_mean")
            neg_mean[u] = fresh_neg_mean
            if NEGG:
                nc.gpsimd.tensor_scalar(out=neg_mean[u][:], in0=row_sum[u][:], scalar1=-1.0 / D, scalar2=0.0, op0=ALU.mult, op1=ALU.add)
            else:
                nc.scalar.activation(out=neg_mean[u][:], in_=row_sum[u][:], func=ACT.Copy, scale=-1.0 / D)

        def invert(u):
            if ARS:
                return
            fresh_rstd = stats.tile([P, tiles_of(u)], F32, tag="rstd")
            rstd[u] = fresh_rstd
            nc.vector.reciprocal(out=rstd[u][:], in_=std[u][:])

        def scale_mean(u):
            fresh_offset = stats.tile([P, tiles_of(u)], F32, tag="offset")
            offset[u] = fresh_offset
            for j in range(tiles_of(u)):
                if NORM(u, j) == "S":
                    nc.scalar.activation(out=offset[u][:, j : j + 1], in_=neg_mean[u][:, j : j + 1], func=ACT.Copy, scale=rstd[u][:, j : j + 1])

        def normalise(u, j):
            tile = residual[u][:, j, :]
            if NORM(u, j) == "S":
                nc.scalar.activation(
                    out=tile, in_=tile, func=ACT.Identity, scale=rstd[u][:, j : j + 1], bias=offset[u][:, j : j + 1]
                )
            else:
                (nc.vector if NORM(u, j) == "V" else nc.gpsimd).tensor_scalar(
                    out=tile,
                    in0=tile,
                    scalar1=neg_mean[u][:, j : j + 1],
                    scalar2=rstd[u][:, j : j + 1],
                    op0=ALU.add,
                    op1=ALU.mult,
                )

        def m_transpose(u, k):
            tiles = tiles_of(u)
            tokens = tiles * P
            if k == 0:
                fresh_m_planes = work.tile([P, PACK, tokens], BF16, tag="planes", bufs=PBUFS)
                m_planes[u] = fresh_m_planes
            group = BANK // tokens
            held["t"] += 1
            assert held["t"] <= PST
            bank = ps_t.tile([P, group, tiles, P], F32, tag="t")
            m_bank[u, k] = bank
            for i in range(group):
                c = k * group + i
                for j in range(tiles):
                    nc.tensor.transpose(bank[:, i, j, :], residual[u][:, j, c * P : (c + 1) * P], ident_f32[:])

        def affine(u, k):
            held["t"] -= 1
            tiles = tiles_of(u)
            group = BANK // (tiles * P)
            bank = m_bank[u, k]
            for i in range(group):
                c = k * group + i
                if AFF(u, c) == "S":
                    nc.scalar.activation(
                        out=m_planes[u][:, c, :],
                        in_=bank[:, i, :, :].rearrange("p j t -> p (j t)"),
                        func=ACT.Identity,
                        bias=shift[:, c : c + 1],
                        scale=gain[:, c : c + 1],
                    )
                else:
                    nc.vector.tensor_scalar(
                        out=m_planes[u][:, c, :],
                        in0=bank[:, i, :, :].rearrange("p j t -> p (j t)"),
                        scalar1=gain[:, c : c + 1],
                        scalar2=shift[:, c : c + 1],
                        op0=ALU.mult,
                        op1=ALU.add,
                    )

        def m_interleave(u, k):
            tokens = tiles_of(u) * P
            n = INTN(u)
            if k == 0:
                fresh_m_grouped = work.tile([P, tokens, PACK], BF16, tag="grouped_m", bufs=GBUFS, align_bytes=64)
                m_grouped[u] = fresh_m_grouped
            a, b = k * tokens // n, (k + 1) * tokens // n
            target = m_grouped[u][:, a:b, :].rearrange("p (w i) c -> p w c i", i=4)
            source = m_planes[u][:, :, a:b].rearrange("p c (w i) -> p w c i", i=4)
            if INTER(u, k) == "V":
                nc.vector.tensor_copy(out=target, in_=source)
            elif INTER(u, k) == "S":
                nc.scalar.copy(out=target, in_=source)
            else:
                nc.gpsimd.tensor_scalar(out=target, in0=source, scalar1=1.0, scalar2=0.0, op0=ALU.mult, op1=ALU.add)

        def m_quantise(u):
            tokens = tiles_of(u) * P
            fresh_m_codes = work.tile([P, tokens], U32, tag="m_codes", align_bytes=64)
            m_codes[u] = fresh_m_codes
            fresh_m_scales = work.tile([P, tokens], U8, tag="m_scales", align_bytes=64)
            m_scales[u] = fresh_m_scales
            quantise(m_grouped[u][:], m_codes[u][:], m_scales[u][:])

        def feed_forward(u, k):
            j, h = divmod(k, 2)
            held["mx"] += 1
            assert held["mx"] <= 8 - PST
            acc = ps_mx.tile([P, BANK], F32, tag="mx")
            nc.tensor.matmul_mx(
                out=acc[:],
                lhsT=m_codes[u][:, j * P : (j + 1) * P].bitcast(FP8X4),
                lhsT_scale=m_scales[u][:, j * P : (j + 1) * P],
                rhs=ff1_codes[h][:].bitcast(FP8X4),
                rhs_scale=ff1_scales[h][:],
                start=True,
                stop=True,
            )
            acc_bank[u, k] = acc

        def add_bias(u, k):
            held["mx"] -= 1
            j, h = divmod(k, 2)
            acc = acc_bank[u, k]
            if h == 0:
                fresh_result = results.tile([P, F], F32, tag="result")
                result[u, j] = fresh_result
            nc.vector.tensor_tensor(
                out=result[u, j][:, h * BANK : (h + 1) * BANK],
                in0=acc[:],
                in1=bias_all[:, h * BANK : (h + 1) * BANK],
                op=ALU.add,
            )

        def relu(u, k):
            n = RELUN(u)
            j, q = divmod(k, n)
            tile = result[u, j][:, q * F // n : (q + 1) * F // n]
            which = RELU(u, j, q)
            if which == "S":
                nc.scalar.activation(out=tile, in_=tile, func=ACT.Relu)
            elif which == "V":
                nc.vector.tensor_scalar_max(out=tile, in0=tile, scalar1=0.0)
            else:
                nc.gpsimd.tensor_scalar(out=tile, in0=tile, scalar1=F32_MAX, scalar2=0.0, op0=ALU.min, op1=ALU.max)

        def store(u, k):
            s, at, tiles = PIECES[u]
            n = RELUN(u)
            j, q = divmod(k, n)
            cols = slice(q * F // n, (q + 1) * F // n)
            nc.sync.dma_start(
                out=out[s, at : at + tiles * P, :].rearrange("(p j) f -> p j f", j=tiles)[:, j, cols],
                in_=result[u, j][:, cols],
            )

        def prepare_vectors():
            nc.vector.tensor_copy(out=gain[:], in_=gain_rows[:])
            nc.vector.tensor_copy(out=shift[:], in_=shift_rows[:])

        def prepare_bias(h):
            assert held["mx"] < 8 - PST
            bias_bank = ps_mx.tile([P, BANK], F32, tag="mx")
            nc.tensor.matmul(
                out=bias_bank[:], lhsT=ones[:], rhs=bias_row[:, h * BANK : (h + 1) * BANK], start=True, stop=True
            )
            BIASCOPY(nc)(out=bias_all[:, h * BANK : (h + 1) * BANK], in_=bias_bank[:])

        def prepare_ff1(k):
            h, i = divmod(k, 2)
            transpose_pair(ff1_sb[:, 4 * h : 4 * h + 4, :], 2 * i, ff1_grouped[h], FF1COPY(nc, k))

        def quantise_ff1(h):
            quantise(ff1_grouped[h][:], ff1_codes[h][:], ff1_scales[h][:])

        atoms = []
        START = [sum(p[2] for p in PIECES[:u]) for u in range(UNITS + 1)]

        def add(u, at, spread, n, make):
            tiles = tiles_of(u)
            for k in range(n):
                atoms.append((START[u] + tiles * (at + spread * (k + 0.5) / n), len(atoms), make(k)))

        def add_at(at, spread, n, make):
            for k in range(n):
                atoms.append((at + spread * (k + 0.5) / n, len(atoms), make(k)))

        for u in range(UNITS):
            n = tiles_of(u)
            banks = n * D // BANK
            add(u, O["XT"], 0.5, (n + 1) // 2, lambda k, u=u: lambda: ax_transpose(u, k))
            add(u, O["XC"], 0.5, (n + 1) // 2, lambda k, u=u: lambda: ax_copy(u, k))
            add(u, O["Q1"], 0, 1, lambda k, u=u: lambda: ax_quantise(u))
            add(u, O["PM"], O["PM1"], n, lambda k, u=u: lambda: project(u, k))
            add(u, O["T"], 1, n, lambda k, u=u: lambda: add_residual(u, k))
            add(u, O["SQ"], 1, n, lambda k, u=u: lambda: square(u, k))
            add(u, O["RS"], 0, 1, lambda k, u=u: lambda: negate_mean(u))
            add(u, O["RS"], 0, 1, lambda k, u=u: lambda: finish_statistics(u))
            if not ARS:
                add(u, O["RC"], 0, 1, lambda k, u=u: lambda: invert(u))
            if any(NORM(u, j) == "S" for j in range(n)):
                add(u, O["N0"], 0, 1, lambda k, u=u: lambda: scale_mean(u))
            add(u, O["N0"], O["N1"], n, lambda k, u=u: lambda: normalise(u, k))
            add(u, O["MT"], O["MT1"], banks, lambda k, u=u: lambda: m_transpose(u, k))
            add(u, O["AF"], O["AF1"], banks, lambda k, u=u: lambda: affine(u, k))
            add(u, O["I"], 0, INTN(u), lambda k, u=u: lambda: m_interleave(u, k))
            add(u, O["Q2"], 0, 1, lambda k, u=u: lambda: m_quantise(u))
            add(u, O["FM"], O["FM1"], 2 * n, lambda k, u=u: lambda: feed_forward(u, k))
            add(u, O["B"], 1, 2 * n, lambda k, u=u: lambda: add_bias(u, k))
            add(u, O["R"], 1, n * RELUN(u), lambda k, u=u: lambda: relu(u, k))
            add(u, O["R"], 1, n * RELUN(u), lambda k, u=u: lambda: store(u, k))
        add_at(O["KB"], 0, 1, lambda k: prepare_vectors)
        add_at(O["KB"], 1, 2, lambda k: lambda: prepare_bias(k))
        add_at(O["KP"], 2, 4, lambda k: lambda: prepare_ff1(k))
        add_at(O["KP"] + 2.2, 0.6, 2, lambda k: lambda: quantise_ff1(k))
        for key, order, run in sorted(atoms, key=lambda a: (a[0], a[1])):
            run()
